import numpy as np
import ml_dtypes


def mxq(x, axis, fmt="e4m3"):
    dtype, down = {"e4m3": (ml_dtypes.float8_e4m3fn, 7), "e5m2": (ml_dtypes.float8_e5m2, 14)}[fmt]
    v = np.moveaxis(np.asarray(x, np.float32).astype(ml_dtypes.bfloat16).astype(np.float64), axis, -1)
    blocks = v.reshape(v.shape[:-1] + (-1, 32))
    amax = np.abs(blocks).max(-1, keepdims=True)
    byte = np.maximum(np.where(amax > 0, np.frexp(amax)[1] - 1 + 127, 0) - down, 1)
    scale = np.exp2(byte - 127.0)
    codes = (blocks / scale).astype(np.float32).astype(dtype).astype(np.float64)
    return np.moveaxis((codes * scale).reshape(v.shape), -1, axis)


WIDE = False


def mx_kscale(k):
    if not WIDE:
        return np.ones(k)
    levels = np.array([30, -30])
    if k % 512:
        return np.exp2(np.random.permutation(np.resize(levels, k // 32))).repeat(32)
    a = np.empty((k // 512, 16))
    for p in range(k // 512):
        a[p, :8] = np.random.permutation(np.resize(levels, 8))
        for g in range(8):
            far = levels[np.abs(levels - a[p, g]) >= 10]
            a[p, g + 8] = far[np.random.randint(len(far))]
    return np.exp2(a.ravel()).repeat(32)


BF16 = ml_dtypes.bfloat16


def bf(x):
    return np.asarray(x, np.float32).astype(BF16)


def f64(x):
    return np.asarray(x).astype(np.float64)


B, S, H, NH, NKV, HD = 1, 512, 2048, 16, 4, 128
HALF = HD // 2
THETA = 10000.0


def rope_tables():
    inv_freq = 1.0 / THETA ** (np.arange(0, HD, 2) / HD)
    freqs = np.arange(S)[:, None] * inv_freq[None, :]
    emb = np.concatenate([freqs, freqs], axis=-1)
    return np.cos(emb), np.sin(emb)


def rotate_half(u):
    return np.concatenate([-u[..., HALF:], u[..., :HALF]], axis=-1)


def heads(y, n):
    return y.reshape(B, S, n, HD).transpose(0, 2, 1, 3)


def setup_inputs():
    s = mx_kscale(H)
    return {"x": bf(np.random.standard_normal((B, S, H)) * s),
            "Wq": bf(np.random.standard_normal((NH * HD, H)) * 1.25 / np.sqrt(H) / s[None, :]),
            "Wk": bf(np.random.standard_normal((NKV * HD, H)) * 1.25 / np.sqrt(H) / s[None, :]),
            "Wv": bf(np.random.standard_normal((NKV * HD, H)) / np.sqrt(H) / s[None, :])}


def reference(x, Wq, Wk, Wv):
    xq = mxq(f64(x), 2, "e5m2")
    q = heads(xq @ mxq(f64(Wq), 1, "e5m2").T, NH)
    k = heads(xq @ mxq(f64(Wk), 1, "e5m2").T, NKV)
    v = heads(xq @ mxq(f64(Wv), 1, "e5m2").T, NKV)
    cos, sin = rope_tables()
    q_rot = q * cos + rotate_half(q) * sin
    k_rot = k * cos + rotate_half(k) * sin
    return q_rot, k_rot, v

@@ -1,0 +1,258 @@
+import math
+from contextlib import ExitStack
+
+import concourse.mybir as mybir
+from concourse.masks import make_identity
+
+S, H, NH, NKV, HD = 512, 2048, 16, 4, 128
+FLOPS = 2 * S * H * (NH + 2 * NKV) * HD
+
+F32 = mybir.dt.float32
+BF16 = mybir.dt.bfloat16
+I32 = mybir.dt.int32
+U32 = mybir.dt.uint32
+U8 = mybir.dt.uint8
+E5X4 = mybir.dt.float8_e5m2_x4
+ALU = mybir.AluOpType
+ACT = mybir.ActivationFunctionType
+
+P = 128
+PASSES = 4
+GROUPS = 6
+N_T = 2 + 2 * GROUPS
+N_MM = 2 * GROUPS
+LAG = 4
+HALF = 64
+RATIO = 10000.0 ** (-1.0 / 64.0)
+TWO_PI = 2.0 * math.pi
+C1 = 6.28125
+C2 = TWO_PI - C1
+
+
+def tile_efficientattention_pa_kernel(tc, x, Wq, Wk, Wv, out_0, out_1, out_2):
+    nc = tc.nc
+    with ExitStack() as ctx:
+        ctx.enter_context(tc.manual_schedule())
+        const = ctx.enter_context(tc.tile_pool(name="const", bufs=1))
+        raw = ctx.enter_context(tc.tile_pool(name="raw", bufs=1))
+        stage = ctx.enter_context(tc.tile_pool(name="stage", bufs=4))
+        wq_pool = ctx.enter_context(tc.tile_pool(name="wq_pool", bufs=3))
+        work = ctx.enter_context(tc.tile_pool(name="work", bufs=2))
+        psum_t = ctx.enter_context(tc.psum_pool(name="psum_t", bufs=4))
+        psum_m = ctx.enter_context(tc.psum_pool(name="psum_m", bufs=4))
+
+        xv = x.flatten_outer_dims().rearrange("(r a) k -> r a k", a=4)
+        x_raw = []
+        for g in range(PASSES):
+            t = raw.tile([P, 4, 512], BF16, name="x_raw%d" % g, tag="x_raw%d" % g)
+            nc.sync.dma_start(out=t[:], in_=xv[:, :, 512 * g : 512 * (g + 1)])
+            x_raw.append(t)
+        w_raw = []
+        for n in range(GROUPS):
+            if n < 4:
+                src = Wq[512 * n : 512 * (n + 1), :]
+            elif n == 4:
+                src = Wk
+            else:
+                src = Wv
+            wv = src.rearrange("(i d) k -> d i k", i=4)
+            for gp in range(2):
+                t = raw.tile([P, 4, 1024], BF16, name="w_raw%d_%d" % (n, gp), tag="w_raw%d_%d" % (n, gp))
+                nc.sync.dma_start(out=t[:], in_=wv[:, :, 1024 * gp : 1024 * (gp + 1)])
+                w_raw.append(t)
+
+        ident = const.tile([P, P], F32, name="ident", tag="ident")
+        make_identity(nc, ident[:])
+        zero1 = const.tile([P, 1], F32, name="zero1", tag="zero1")
+        nc.vector.memset(zero1[:], 0.0)
+        warm = const.tile([P, 1], F32, name="warm", tag="warm")
+        nc.scalar.activation(out=warm[:], in_=zero1[:], func=ACT.Sin)
+
+        pos_i = const.tile([P, 4], I32, name="pos_i", tag="pos_i")
+        nc.gpsimd.iota(pos_i[:], pattern=[[1, 4]], base=0, channel_multiplier=4)
+        pos = const.tile([P, 4], F32, name="pos", tag="pos")
+        nc.vector.tensor_copy(out=pos[:], in_=pos_i[:])
+        ones = const.tile([P, 8], F32, name="ones", tag="ones")
+        nc.vector.memset(ones[:], 1.0)
+        fa = const.tile([P, 8, 8], F32, name="fa", tag="fa")
+        fb = const.tile([P, 8, 8], F32, name="fb", tag="fb")
+        for j in range(8):
+            nc.vector.tensor_scalar(out=fa[:, j, :], in0=ones[:], scalar1=RATIO ** (8 * j), scalar2=None, op0=ALU.mult)
+            nc.vector.tensor_scalar(out=fb[:, :, j], in0=ones[:], scalar1=RATIO ** j, scalar2=None, op0=ALU.mult)
+        freq = const.tile([P, HALF], F32, name="freq", tag="freq")
+        nc.vector.tensor_tensor(
+            out=freq[:], in0=fa[:].rearrange("p a b -> p (a b)"), in1=fb[:].rearrange("p a b -> p (a b)"), op=ALU.mult
+        )
+        ang = const.tile([P, 4, HALF], F32, name="ang", tag="ang")
+        for a in range(4):
+            nc.vector.tensor_scalar(out=ang[:, a, :], in0=freq[:], scalar1=pos[:, a : a + 1], scalar2=None, op0=ALU.mult)
+        angf = ang[:].rearrange("p a j -> p (a j)")
+        turns_i = const.tile([P, 4 * HALF], I32, name="turns_i", tag="turns_i")
+        nc.vector.tensor_scalar(out=turns_i[:], in0=angf, scalar1=1.0 / TWO_PI, scalar2=None, op0=ALU.mult)
+        turns = const.tile([P, 4 * HALF], F32, name="turns", tag="turns")
+        nc.vector.tensor_copy(out=turns[:], in_=turns_i[:])
+        r1 = const.tile([P, 4 * HALF], F32, name="r1", tag="r1")
+        nc.vector.scalar_tensor_tensor(out=r1[:], in0=turns[:], scalar=-C1, in1=angf, op0=ALU.mult, op1=ALU.add)
+        r2 = const.tile([P, 4 * HALF], F32, name="r2", tag="r2")
+        nc.vector.scalar_tensor_tensor(out=r2[:], in0=turns[:], scalar=-C2, in1=r1[:], op0=ALU.mult, op1=ALU.add)
+        m1 = const.tile([P, 4 * HALF], F32, name="m1", tag="m1")
+        nc.vector.tensor_scalar(out=m1[:], in0=r2[:], scalar1=math.pi, scalar2=-TWO_PI, op0=ALU.is_gt, op1=ALU.mult)
+        r3 = const.tile([P, 4 * HALF], F32, name="r3", tag="r3")
+        nc.vector.tensor_tensor(out=r3[:], in0=r2[:], in1=m1[:], op=ALU.add)
+        m2 = const.tile([P, 4 * HALF], F32, name="m2", tag="m2")
+        nc.vector.tensor_scalar(out=m2[:], in0=r3[:], scalar1=-math.pi, scalar2=TWO_PI, op0=ALU.is_lt, op1=ALU.mult)
+        r4 = const.tile([P, 4, HALF], F32, name="r4", tag="r4")
+        r4f = r4[:].rearrange("p a j -> p (a j)")
+        nc.vector.tensor_tensor(out=r4f, in0=r3[:], in1=m2[:], op=ALU.add)
+        absr = const.tile([P, 4, HALF], F32, name="absr", tag="absr")
+        nc.vector.scalar_tensor_tensor(
+            out=absr[:].rearrange("p a j -> p (a j)"), in0=r4f, scalar=-1.0, in1=r4f, op0=ALU.mult, op1=ALU.max
+        )
+        sin_pm = const.tile([P, 4, 2, HALF], F32, name="sin_pm", tag="sin_pm")
+        cos_t = const.tile([P, 4, HALF], F32, name="cos_t", tag="cos_t")
+
+        def finish_tables():
+            nc.scalar.activation(out=sin_pm[:, :, 0, :], in_=r4[:], func=ACT.Sin)
+            nc.scalar.activation(out=sin_pm[:, :, 1, :], in_=r4[:], func=ACT.Sin, scale=-1.0)
+            nc.scalar.activation(out=cos_t[:], in_=absr[:], func=ACT.Sin, scale=-1.0, bias=math.pi / 2.0)
+
+        x_codes = const.tile([P, PASSES, 512], U32, name="x_codes", tag="x_codes", align_bytes=64)
+        x_scales = const.tile([P, PASSES, 512], U8, name="x_scales", tag="x_scales", align_bytes=64)
+        w_codes = {}
+        w_scales = {}
+        o_tiles = {}
+        prods = {}
+
+        def words(step, gl, i, u):
+            if step < 2:
+                return x_raw[2 * step + gl][:].bitcast(F32)[:, i, u:256:2]
+            return w_raw[step - 2][:].bitcast(F32)[:, i, 256 * gl + u : 256 * (gl + 1) : 2]
+
+        def transposes(step):
+            banks = []
+            for gl in range(2):
+                for ip in range(2):
+                    tp = psum_t.tile([P, 2, 2, P], F32, name="tp", tag="tp")
+                    for il in range(2):
+                        for u in range(2):
+                            nc.tensor.transpose(tp[:, il, u, :], words(step, gl, 2 * ip + il, u), ident[:])
+                    banks.append(tp)
+            return banks
+
+        def copies(step, banks):
+            grouped = []
+            for gl in range(2):
+                gt = stage.tile([P, 2048], BF16, name="grouped", tag="grouped", align_bytes=64)
+                gw = gt[:].bitcast(F32).rearrange("p (i r u) -> p i r u", i=4, u=2)
+                for ip in range(2):
+                    src = banks[2 * gl + ip][:].rearrange("p i u r -> p i r u")
+                    if step <= LAG and ip == 1 and gl == 1:
+                        nc.vector.tensor_copy(out=gw[:, 2 * ip : 2 * ip + 2], in_=src)
+                    else:
+                        nc.scalar.copy(out=gw[:, 2 * ip : 2 * ip + 2], in_=src)
+                grouped.append(gt)
+            return grouped
+
+        def quantize(step, grouped):
+            for gl in range(2):
+                if step < 2:
+                    codes, scales, g = x_codes, x_scales, 2 * step + gl
+                else:
+                    n = (step - 2) // 2
+                    g = 2 * ((step - 2) % 2) + gl
+                    if g == 0:
+                        wc = wq_pool.tile([P, PASSES, 512], U32, name="w_codes", tag="w_codes", align_bytes=64)
+                        ws = wq_pool.tile([P, PASSES, 512], U8, name="w_scales", tag="w_scales", align_bytes=64)
+                        w_codes[n] = wc
+                        w_scales[n] = ws
+                    codes, scales = w_codes[n], w_scales[n]
+                nc.vector.quantize_mx(out=codes[:, g, :].bitcast(E5X4), scales=scales[:, g, :], in_=grouped[gl][:])
+
+        def matmuls(mm):
+            n, ap = mm // 2, mm % 2
+            accs = []
+            for al in range(2):
+                a = 2 * ap + al
+                acc = psum_m.tile([P, 512], F32, name="acc", tag="acc")
+                for g in range(PASSES):
+                    nc.tensor.matmul_mx(
+                        out=acc[:],
+                        lhsT=x_codes[:, g, P * a : P * (a + 1)].bitcast(E5X4),
+                        lhsT_scale=x_scales[:, g, P * a : P * (a + 1)],
+                        rhs=w_codes[n][:, g, :].bitcast(E5X4),
+                        rhs_scale=w_scales[n][:, g, :],
+                        start=(g == 0),
+                        stop=(g == PASSES - 1),
+                    )
+                accs.append(acc)
+            return accs
+
+        def out_view(n):
+            if n < 4:
+                return out_0.rearrange("b h (r a) d -> r (b h) a d", a=4)[:, 4 * n : 4 * n + 4]
+            if n == 4:
+                return out_1.rearrange("b h (r a) d -> r (b h) a d", a=4)
+            return out_2.rearrange("b h (r a) d -> r (b h) a d", a=4)
+
+        def products(mm, accs):
+            n, ap = mm // 2, mm % 2
+            if ap == 0:
+                ot = work.tile([P, 4, 4, HD], F32, name="o_tile", tag="o_tile")
+                o_tiles[n] = ot
+            if n == GROUPS - 1:
+                nc.scalar.copy(out=o_tiles[n][:, :, 2 * ap, :], in_=accs[0][:].rearrange("p (h d) -> p h d", h=4))
+                nc.vector.tensor_copy(out=o_tiles[n][:, :, 2 * ap + 1, :], in_=accs[1][:].rearrange("p (h d) -> p h d", h=4))
+                nc.sync.dma_start(
+                    out=out_view(n)[:, :, 2 * ap : 2 * ap + 2, :].rearrange("r h a d -> r h (a d)"),
+                    in_=o_tiles[n][:, :, 2 * ap : 2 * ap + 2, :].rearrange("p h a d -> p h (a d)"),
+                )
+                return
+            pc = work.tile([P, 2, 512], F32, name="prod_cos", tag="prod_cos")
+            ps = work.tile([P, 2, 512], F32, name="prod_sin", tag="prod_sin")
+            for al in range(2):
+                a = 2 * ap + al
+                nc.vector.tensor_tensor(
+                    out=pc[:, al, :].rearrange("p (e j) -> p e j", j=HALF),
+                    in0=accs[al][:].rearrange("p (e j) -> p e j", j=HALF),
+                    in1=cos_t[:, a, :].unsqueeze(1).to_broadcast([P, 8, HALF]),
+                    op=ALU.mult,
+                )
+                nc.vector.tensor_tensor(
+                    out=ps[:, al, :].rearrange("p (h d) -> p h d", d=HD),
+                    in0=accs[al][:].rearrange("p (h d) -> p h d", d=HD),
+                    in1=sin_pm[:, a, :, :].rearrange("p t j -> p (t j)").unsqueeze(1).to_broadcast([P, 4, HD]),
+                    op=ALU.mult,
+                )
+            prods[mm] = (pc, ps)
+
+        def sums(mm):
+            n, ap = mm // 2, mm % 2
+            if mm < 0 or n == GROUPS - 1:
+                return
+            pc, ps = prods[mm]
+            ov = o_tiles[n][:].rearrange("p h a (t j) -> p a h t j", t=2)
+            pcv = pc[:].rearrange("p a (h t j) -> p a h t j", h=4, t=2)
+            psv = ps[:].rearrange("p a (h t j) -> p a h t j", h=4, t=2)
+            for t in range(2):
+                nc.vector.tensor_tensor(
+                    out=ov[:, 2 * ap : 2 * ap + 2, :, t, :], in0=pcv[:, :, :, t, :], in1=psv[:, :, :, 1 - t, :], op=ALU.add
+                )
+            if ap == 1:
+                nc.sync.dma_start(
+                    out=out_view(n).rearrange("r h a d -> r h (a d)"),
+                    in_=o_tiles[n][:].rearrange("p h a d -> p h (a d)"),
+                )
+
+        for step in range(N_MM + LAG):
+            mm = step - LAG
+            if step < N_T:
+                banks = transposes(step)
+                grouped = copies(step, banks)
+            if step == 1:
+                finish_tables()
+            sums(mm - 1)
+            if step < N_T:
+                quantize(step, grouped)
+            if mm >= 0:
+                accs = matmuls(mm)
+                products(mm, accs)

@@ -207,8 +207,8 @@ def tile_efficientattention_pa_kernel(tc, x, Wq, Wk, Wv, out_0, out_1, out_2):
                     in_=o_tiles[n][:, :, 2 * ap : 2 * ap + 2, :].rearrange("p h a d -> p h (a d)"),
                 )
                 return
-            pc = work.tile([P, 2, 512], F32, name="prod_cos", tag="prod_cos")
-            ps = work.tile([P, 2, 512], F32, name="prod_sin", tag="prod_sin")
+            pc = work.tile([P, 2, 512], F32, name="prod_cos", tag="prod_cos", bufs=3)
+            ps = work.tile([P, 2, 512], F32, name="prod_sin", tag="prod_sin", bufs=3)
             for al in range(2):
                 a = 2 * ap + al
                 nc.vector.tensor_tensor(
@@ -234,7 +234,7 @@ def tile_efficientattention_pa_kernel(tc, x, Wq, Wk, Wv, out_0, out_1, out_2):
             pcv = pc[:].rearrange("p a (h t j) -> p a h t j", h=4, t=2)
             psv = ps[:].rearrange("p a (h t j) -> p a h t j", h=4, t=2)
             for t in range(2):
-                nc.vector.tensor_tensor(
+                nc.gpsimd.tensor_tensor(
                     out=ov[:, 2 * ap : 2 * ap + 2, :, t, :], in0=pcv[:, :, :, t, :], in1=psv[:, :, :, 1 - t, :], op=ALU.add
                 )
             if ap == 1:
@@ -250,9 +250,9 @@ def tile_efficientattention_pa_kernel(tc, x, Wq, Wk, Wv, out_0, out_1, out_2):
                 grouped = copies(step, banks)
             if step == 1:
                 finish_tables()
-            sums(mm - 1)
             if step < N_T:
                 quantize(step, grouped)
             if mm >= 0:
                 accs = matmuls(mm)
                 products(mm, accs)
+                sums(mm)

@@ -22,6 +22,9 @@ GROUPS = 6
 N_T = 2 + 2 * GROUPS
 N_MM = 2 * GROUPS
 LAG = 4
+RAW_BUFS = 8
+R0 = 6
+R_TILES = 3
 HALF = 64
 RATIO = 10000.0 ** (-1.0 / 64.0)
 TWO_PI = 2.0 * math.pi
@@ -34,32 +37,39 @@ def tile_efficientattention_pa_kernel(tc, x, Wq, Wk, Wv, out_0, out_1, out_2):
     with ExitStack() as ctx:
         ctx.enter_context(tc.manual_schedule())
         const = ctx.enter_context(tc.tile_pool(name="const", bufs=1))
-        raw = ctx.enter_context(tc.tile_pool(name="raw", bufs=1))
-        stage = ctx.enter_context(tc.tile_pool(name="stage", bufs=4))
+        raw = ctx.enter_context(tc.tile_pool(name="raw", bufs=RAW_BUFS))
+        stage = ctx.enter_context(tc.tile_pool(name="stage", bufs=3))
         wq_pool = ctx.enter_context(tc.tile_pool(name="wq_pool", bufs=3))
         work = ctx.enter_context(tc.tile_pool(name="work", bufs=2))
         psum_t = ctx.enter_context(tc.psum_pool(name="psum_t", bufs=4))
         psum_m = ctx.enter_context(tc.psum_pool(name="psum_m", bufs=4))
 
         xv = x.flatten_outer_dims().rearrange("(r a) k -> r a k", a=4)
-        x_raw = []
-        for g in range(PASSES):
-            t = raw.tile([P, 4, 512], BF16, name="x_raw%d" % g, tag="x_raw%d" % g)
-            nc.sync.dma_start(out=t[:], in_=xv[:, :, 512 * g : 512 * (g + 1)])
-            x_raw.append(t)
-        w_raw = []
-        for n in range(GROUPS):
+        raw_tiles = {}
+
+        def load(step):
+            t = raw.tile([P, 4, 1024], BF16, name="raw_t", tag="raw_t")
+            raw_tiles[step] = t
+            if step == 0:
+                nc.sync.dma_start(out=t[:, 0:2, 0:512], in_=xv[:, 0:2, 0:512])
+                nc.sync.dma_start(out=t[:, 2:4, 0:512], in_=xv[:, 2:4, 0:512])
+                nc.sync.dma_start(out=t[:, :, 512:1024], in_=xv[:, :, 512:1024])
+                return
+            if step == 1:
+                nc.sync.dma_start(out=t[:, :, 0:512], in_=xv[:, :, 1024:1536])
+                nc.sync.dma_start(out=t[:, :, 512:1024], in_=xv[:, :, 1536:2048])
+                return
+            n, gp = (step - 2) // 2, (step - 2) % 2
             if n < 4:
                 src = Wq[512 * n : 512 * (n + 1), :]
             elif n == 4:
                 src = Wk
             else:
                 src = Wv
-            wv = src.rearrange("(i d) k -> d i k", i=4)
-            for gp in range(2):
-                t = raw.tile([P, 4, 1024], BF16, name="w_raw%d_%d" % (n, gp), tag="w_raw%d_%d" % (n, gp))
-                nc.sync.dma_start(out=t[:], in_=wv[:, :, 1024 * gp : 1024 * (gp + 1)])
-                w_raw.append(t)
+            nc.sync.dma_start(out=t[:], in_=src.rearrange("(i d) k -> d i k", i=4)[:, :, 1024 * gp : 1024 * (gp + 1)])
+
+        for step in range(RAW_BUFS):
+            load(step)
 
         ident = const.tile([P, P], F32, name="ident", tag="ident")
         make_identity(nc, ident[:])
@@ -123,10 +133,22 @@ def tile_efficientattention_pa_kernel(tc, x, Wq, Wk, Wv, out_0, out_1, out_2):
         o_tiles = {}
         prods = {}
 
+        ro_tiles = {}
+
+        def reorder(step):
+            if step < R0 or step >= N_T:
+                return
+            ro = stage.tile([P, R_TILES, 512], F32, name="ro", tag="ro")
+            ro_tiles[step] = ro
+            nc.scalar.copy(
+                out=ro[:].rearrange("p i (g u m) -> p (i g) u m", g=2, u=2),
+                in_=raw_tiles[step][:].bitcast(F32)[:, 0:R_TILES, :].rearrange("p i (g m u) -> p (i g) u m", g=2, u=2),
+            )
+
         def words(step, gl, i, u):
-            if step < 2:
-                return x_raw[2 * step + gl][:].bitcast(F32)[:, i, u:256:2]
-            return w_raw[step - 2][:].bitcast(F32)[:, i, 256 * gl + u : 256 * (gl + 1) : 2]
+            if step >= R0 and i < R_TILES:
+                return ro_tiles[step][:, i, 256 * gl + 128 * u : 256 * gl + 128 * (u + 1)]
+            return raw_tiles[step][:].bitcast(F32)[:, i, 256 * gl + u : 256 * (gl + 1) : 2]
 
         def transposes(step):
             banks = []
@@ -140,33 +162,34 @@ def tile_efficientattention_pa_kernel(tc, x, Wq, Wk, Wv, out_0, out_1, out_2):
             return banks
 
         def copies(step, banks):
-            grouped = []
+            gt = stage.tile([P, 4096], BF16, name="grouped", tag="grouped", align_bytes=64)
+            gw = gt[:].bitcast(F32).rearrange("p (g i r u) -> p g i r u", g=2, i=4, u=2)
             for gl in range(2):
-                gt = stage.tile([P, 2048], BF16, name="grouped", tag="grouped", align_bytes=64)
-                gw = gt[:].bitcast(F32).rearrange("p (i r u) -> p i r u", i=4, u=2)
                 for ip in range(2):
                     src = banks[2 * gl + ip][:].rearrange("p i u r -> p i r u")
                     if step <= LAG and ip == 1 and gl == 1:
-                        nc.vector.tensor_copy(out=gw[:, 2 * ip : 2 * ip + 2], in_=src)
+                        nc.vector.tensor_copy(out=gw[:, gl, 2 * ip : 2 * ip + 2], in_=src)
                     else:
-                        nc.scalar.copy(out=gw[:, 2 * ip : 2 * ip + 2], in_=src)
-                grouped.append(gt)
-            return grouped
+                        nc.scalar.copy(out=gw[:, gl, 2 * ip : 2 * ip + 2], in_=src)
+            return gt
 
         def quantize(step, grouped):
-            for gl in range(2):
-                if step < 2:
-                    codes, scales, g = x_codes, x_scales, 2 * step + gl
-                else:
-                    n = (step - 2) // 2
-                    g = 2 * ((step - 2) % 2) + gl
-                    if g == 0:
-                        wc = wq_pool.tile([P, PASSES, 512], U32, name="w_codes", tag="w_codes", align_bytes=64)
-                        ws = wq_pool.tile([P, PASSES, 512], U8, name="w_scales", tag="w_scales", align_bytes=64)
-                        w_codes[n] = wc
-                        w_scales[n] = ws
-                    codes, scales = w_codes[n], w_scales[n]
-                nc.vector.quantize_mx(out=codes[:, g, :].bitcast(E5X4), scales=scales[:, g, :], in_=grouped[gl][:])
+            if step < 2:
+                codes, scales, g0 = x_codes, x_scales, 2 * step
+            else:
+                n = (step - 2) // 2
+                g0 = 2 * ((step - 2) % 2)
+                if g0 == 0:
+                    wc = wq_pool.tile([P, PASSES, 512], U32, name="w_codes", tag="w_codes", align_bytes=64)
+                    ws = wq_pool.tile([P, PASSES, 512], U8, name="w_scales", tag="w_scales", align_bytes=64)
+                    w_codes[n] = wc
+                    w_scales[n] = ws
+                codes, scales = w_codes[n], w_scales[n]
+            nc.vector.quantize_mx(
+                out=codes[:, g0 : g0 + 2, :].rearrange("p g c -> p (g c)").bitcast(E5X4),
+                scales=scales[:, g0 : g0 + 2, :].rearrange("p g c -> p (g c)"),
+                in_=grouped[:],
+            )
 
         def matmuls(mm):
             n, ap = mm // 2, mm % 2
@@ -201,11 +224,9 @@ def tile_efficientattention_pa_kernel(tc, x, Wq, Wk, Wv, out_0, out_1, out_2):
                 o_tiles[n] = ot
             if n == GROUPS - 1:
                 nc.scalar.copy(out=o_tiles[n][:, :, 2 * ap, :], in_=accs[0][:].rearrange("p (h d) -> p h d", h=4))
+                nc.sync.dma_start(out=out_view(n)[:, :, 2 * ap, :], in_=o_tiles[n][:, :, 2 * ap, :])
                 nc.vector.tensor_copy(out=o_tiles[n][:, :, 2 * ap + 1, :], in_=accs[1][:].rearrange("p (h d) -> p h d", h=4))
-                nc.sync.dma_start(
-                    out=out_view(n)[:, :, 2 * ap : 2 * ap + 2, :].rearrange("r h a d -> r h (a d)"),
-                    in_=o_tiles[n][:, :, 2 * ap : 2 * ap + 2, :].rearrange("p h a d -> p h (a d)"),
-                )
+                nc.sync.dma_start(out=out_view(n)[:, :, 2 * ap + 1, :], in_=o_tiles[n][:, :, 2 * ap + 1, :])
                 return
             pc = work.tile([P, 2, 512], F32, name="prod_cos", tag="prod_cos", bufs=3)
             ps = work.tile([P, 2, 512], F32, name="prod_sin", tag="prod_sin", bufs=3)
@@ -233,11 +254,18 @@ def tile_efficientattention_pa_kernel(tc, x, Wq, Wk, Wv, out_0, out_1, out_2):
             ov = o_tiles[n][:].rearrange("p h a (t j) -> p a h t j", t=2)
             pcv = pc[:].rearrange("p a (h t j) -> p a h t j", h=4, t=2)
             psv = ps[:].rearrange("p a (h t j) -> p a h t j", h=4, t=2)
+            last_rope = n == GROUPS - 2
             for t in range(2):
-                nc.gpsimd.tensor_tensor(
+                eng = nc.vector if last_rope else nc.gpsimd
+                eng.tensor_tensor(
                     out=ov[:, 2 * ap : 2 * ap + 2, :, t, :], in0=pcv[:, :, :, t, :], in1=psv[:, :, :, 1 - t, :], op=ALU.add
                 )
-            if ap == 1:
+            if last_rope:
+                nc.sync.dma_start(
+                    out=out_view(n)[:, :, 2 * ap : 2 * ap + 2, :].rearrange("r h a d -> r h (a d)"),
+                    in_=o_tiles[n][:, :, 2 * ap : 2 * ap + 2, :].rearrange("p h a d -> p h (a d)"),
+                )
+            elif ap == 1:
                 nc.sync.dma_start(
                     out=out_view(n).rearrange("r h a d -> r h (a d)"),
                     in_=o_tiles[n][:].rearrange("p h a d -> p h (a d)"),
@@ -248,6 +276,9 @@ def tile_efficientattention_pa_kernel(tc, x, Wq, Wk, Wv, out_0, out_1, out_2):
             if step < N_T:
                 banks = transposes(step)
                 grouped = copies(step, banks)
+                reorder(step + 2)
+                if step + RAW_BUFS < N_T:
+                    load(step + RAW_BUFS)
             if step == 1:
                 finish_tables()
             if step < N_T:

@@ -134,6 +134,11 @@ def tile_efficientattention_pa_kernel(tc, x, Wq, Wk, Wv, out_0, out_1, out_2):
         prods = {}
 
         ro_tiles = {}
+        latch = const.tile([P, 1], U32, name="latch", tag="latch")
+
+        def hold_gpsimd(step):
+            n, g0 = (step - 2) // 2, 2 * ((step - 2) % 2)
+            nc.gpsimd.tensor_copy(out=latch[:], in_=w_codes[n][:, g0 + 1, 511:512])
 
         def reorder(step):
             if step < R0 or step >= N_T:
@@ -283,7 +288,11 @@ def tile_efficientattention_pa_kernel(tc, x, Wq, Wk, Wv, out_0, out_1, out_2):
                 finish_tables()
             if step < N_T:
                 quantize(step, grouped)
+            if 0 <= mm - 1 < 2 * (GROUPS - 2):
+                hold_gpsimd(step)
+                sums(mm - 1)
             if mm >= 0:
                 accs = matmuls(mm)
                 products(mm, accs)
-                sums(mm)
+                if mm // 2 == GROUPS - 2:
+                    sums(mm)

@@ -134,11 +134,6 @@ def tile_efficientattention_pa_kernel(tc, x, Wq, Wk, Wv, out_0, out_1, out_2):
         prods = {}
 
         ro_tiles = {}
-        latch = const.tile([P, 1], U32, name="latch", tag="latch")
-
-        def hold_gpsimd(step):
-            n, g0 = (step - 2) // 2, 2 * ((step - 2) % 2)
-            nc.gpsimd.tensor_copy(out=latch[:], in_=w_codes[n][:, g0 + 1, 511:512])
 
         def reorder(step):
             if step < R0 or step >= N_T:
@@ -225,7 +220,7 @@ def tile_efficientattention_pa_kernel(tc, x, Wq, Wk, Wv, out_0, out_1, out_2):
         def products(mm, accs):
             n, ap = mm // 2, mm % 2
             if ap == 0:
-                ot = work.tile([P, 4, 4, HD], F32, name="o_tile", tag="o_tile")
+                ot = work.tile([P, 4, 4, HD], F32, name="o_tile", tag="o_tile", bufs=3)
                 o_tiles[n] = ot
             if n == GROUPS - 1:
                 nc.scalar.copy(out=o_tiles[n][:, :, 2 * ap, :], in_=accs[0][:].rearrange("p (h d) -> p h d", h=4))
@@ -239,14 +234,14 @@ def tile_efficientattention_pa_kernel(tc, x, Wq, Wk, Wv, out_0, out_1, out_2):
                 a = 2 * ap + al
                 nc.vector.tensor_tensor(
                     out=pc[:, al, :].rearrange("p (e j) -> p e j", j=HALF),
-                    in0=accs[al][:].rearrange("p (e j) -> p e j", j=HALF),
-                    in1=cos_t[:, a, :].unsqueeze(1).to_broadcast([P, 8, HALF]),
+                    in0=cos_t[:, a, :].unsqueeze(1).to_broadcast([P, 8, HALF]),
+                    in1=accs[al][:].rearrange("p (e j) -> p e j", j=HALF),
                     op=ALU.mult,
                 )
                 nc.vector.tensor_tensor(
                     out=ps[:, al, :].rearrange("p (h d) -> p h d", d=HD),
-                    in0=accs[al][:].rearrange("p (h d) -> p h d", d=HD),
-                    in1=sin_pm[:, a, :, :].rearrange("p t j -> p (t j)").unsqueeze(1).to_broadcast([P, 4, HD]),
+                    in0=sin_pm[:, a, :, :].rearrange("p t j -> p (t j)").unsqueeze(1).to_broadcast([P, 4, HD]),
+                    in1=accs[al][:].rearrange("p (h d) -> p h d", d=HD),
                     op=ALU.mult,
                 )
             prods[mm] = (pc, ps)
@@ -288,11 +283,7 @@ def tile_efficientattention_pa_kernel(tc, x, Wq, Wk, Wv, out_0, out_1, out_2):
                 finish_tables()
             if step < N_T:
                 quantize(step, grouped)
-            if 0 <= mm - 1 < 2 * (GROUPS - 2):
-                hold_gpsimd(step)
-                sums(mm - 1)
             if mm >= 0:
                 accs = matmuls(mm)
                 products(mm, accs)
-                if mm // 2 == GROUPS - 2:
-                    sums(mm)
+                sums(mm)

@@ -118,13 +118,13 @@ def tile_efficientattention_pa_kernel(tc, x, Wq, Wk, Wv, out_0, out_1, out_2):
         nc.vector.scalar_tensor_tensor(
             out=absr[:].rearrange("p a j -> p (a j)"), in0=r4f, scalar=-1.0, in1=r4f, op0=ALU.mult, op1=ALU.max
         )
-        sin_pm = const.tile([P, 4, 2, HALF], F32, name="sin_pm", tag="sin_pm")
-        cos_t = const.tile([P, 4, HALF], F32, name="cos_t", tag="cos_t")
+        cs_tab = const.tile([P, 4, 2, 2, HALF], F32, name="cs_tab", tag="cs_tab")
 
         def finish_tables():
-            nc.scalar.activation(out=sin_pm[:, :, 0, :], in_=r4[:], func=ACT.Sin)
-            nc.scalar.activation(out=sin_pm[:, :, 1, :], in_=r4[:], func=ACT.Sin, scale=-1.0)
-            nc.scalar.activation(out=cos_t[:], in_=absr[:], func=ACT.Sin, scale=-1.0, bias=math.pi / 2.0)
+            nc.scalar.activation(out=cs_tab[:, :, 1, 0, :], in_=r4[:], func=ACT.Sin)
+            nc.scalar.activation(out=cs_tab[:, :, 1, 1, :], in_=r4[:], func=ACT.Sin, scale=-1.0)
+            for t in range(2):
+                nc.scalar.activation(out=cs_tab[:, :, 0, t, :], in_=absr[:], func=ACT.Sin, scale=-1.0, bias=math.pi / 2.0)
 
         x_codes = const.tile([P, PASSES, 512], U32, name="x_codes", tag="x_codes", align_bytes=64)
         x_scales = const.tile([P, PASSES, 512], U8, name="x_scales", tag="x_scales", align_bytes=64)
@@ -228,39 +228,45 @@ def tile_efficientattention_pa_kernel(tc, x, Wq, Wk, Wv, out_0, out_1, out_2):
                 nc.vector.tensor_copy(out=o_tiles[n][:, :, 2 * ap + 1, :], in_=accs[1][:].rearrange("p (h d) -> p h d", h=4))
                 nc.sync.dma_start(out=out_view(n)[:, :, 2 * ap + 1, :], in_=o_tiles[n][:, :, 2 * ap + 1, :])
                 return
-            pc = work.tile([P, 2, 512], F32, name="prod_cos", tag="prod_cos", bufs=3)
-            ps = work.tile([P, 2, 512], F32, name="prod_sin", tag="prod_sin", bufs=3)
+            pr = work.tile([P, 2, 2, 512], F32, name="prod", tag="prod", bufs=3)
+            prods[mm] = pr
+            last_rope = n == GROUPS - 2
             for al in range(2):
                 a = 2 * ap + al
                 nc.vector.tensor_tensor(
-                    out=pc[:, al, :].rearrange("p (e j) -> p e j", j=HALF),
-                    in0=cos_t[:, a, :].unsqueeze(1).to_broadcast([P, 8, HALF]),
-                    in1=accs[al][:].rearrange("p (e j) -> p e j", j=HALF),
+                    out=pr[:, al, :, :].rearrange("p c (h d) -> p c h d", d=HD),
+                    in0=cs_tab[:, a, :, :, :].rearrange("p c t j -> p c (t j)").unsqueeze(2).to_broadcast([P, 2, 4, HD]),
+                    in1=accs[al][:].rearrange("p (h d) -> p h d", d=HD).unsqueeze(1).to_broadcast([P, 2, 4, HD]),
                     op=ALU.mult,
                 )
-                nc.vector.tensor_tensor(
-                    out=ps[:, al, :].rearrange("p (h d) -> p h d", d=HD),
-                    in0=sin_pm[:, a, :, :].rearrange("p t j -> p (t j)").unsqueeze(1).to_broadcast([P, 4, HD]),
-                    in1=accs[al][:].rearrange("p (h d) -> p h d", d=HD),
-                    op=ALU.mult,
-                )
-            prods[mm] = (pc, ps)
+                if last_rope:
+                    continue
+                if al == 0:
+                    add(nc.gpsimd, mm, 0, 1, 0)
+                else:
+                    add(nc.vector, mm, 0, 1, 1)
+                    add(nc.gpsimd, mm, 1, 2, 0)
+                    add(nc.gpsimd, mm, 1, 2, 1)
+
+        def add(eng, mm, al0, al1, t):
+            n, ap = mm // 2, mm % 2
+            prv = prods[mm][:].rearrange("p a c (h t j) -> p a c h t j", h=4, t=2)
+            ov = o_tiles[n][:].rearrange("p h a (t j) -> p a h t j", t=2)
+            eng.tensor_tensor(
+                out=ov[:, 2 * ap + al0 : 2 * ap + al1, :, t, :],
+                in0=prv[:, al0:al1, 0, :, t, :],
+                in1=prv[:, al0:al1, 1, :, 1 - t, :],
+                op=ALU.add,
+            )
 
         def sums(mm):
             n, ap = mm // 2, mm % 2
             if mm < 0 or n == GROUPS - 1:
                 return
-            pc, ps = prods[mm]
-            ov = o_tiles[n][:].rearrange("p h a (t j) -> p a h t j", t=2)
-            pcv = pc[:].rearrange("p a (h t j) -> p a h t j", h=4, t=2)
-            psv = ps[:].rearrange("p a (h t j) -> p a h t j", h=4, t=2)
             last_rope = n == GROUPS - 2
-            for t in range(2):
-                eng = nc.vector if last_rope else nc.gpsimd
-                eng.tensor_tensor(
-                    out=ov[:, 2 * ap : 2 * ap + 2, :, t, :], in0=pcv[:, :, :, t, :], in1=psv[:, :, :, 1 - t, :], op=ALU.add
-                )
             if last_rope:
+                for t in range(2):
+                    add(nc.vector, mm, 0, 2, t)
                 nc.sync.dma_start(
                     out=out_view(n)[:, :, 2 * ap : 2 * ap + 2, :].rearrange("r h a d -> r h (a d)"),
                     in_=o_tiles[n][:, :, 2 * ap : 2 * ap + 2, :].rearrange("p h a d -> p h (a d)"),

@@ -25,6 +25,7 @@ LAG = 4
 RAW_BUFS = 8
 R0 = 6
 R_TILES = 3
+SPLIT_LAST = 5
 HALF = 64
 RATIO = 10000.0 ** (-1.0 / 64.0)
 TWO_PI = 2.0 * math.pi
@@ -66,7 +67,12 @@ def tile_efficientattention_pa_kernel(tc, x, Wq, Wk, Wv, out_0, out_1, out_2):
                 src = Wk
             else:
                 src = Wv
-            nc.sync.dma_start(out=t[:], in_=src.rearrange("(i d) k -> d i k", i=4)[:, :, 1024 * gp : 1024 * (gp + 1)])
+            view = src.rearrange("(i d) k -> d i k", i=4)[:, :, 1024 * gp : 1024 * (gp + 1)]
+            if step <= SPLIT_LAST:
+                for ip in range(2):
+                    nc.sync.dma_start(out=t[:, 2 * ip : 2 * ip + 2, :], in_=view[:, 2 * ip : 2 * ip + 2, :])
+            else:
+                nc.sync.dma_start(out=t[:], in_=view)
 
         for step in range(RAW_BUFS):
             load(step)
@@ -151,23 +157,26 @@ def tile_efficientattention_pa_kernel(tc, x, Wq, Wk, Wv, out_0, out_1, out_2):
             return raw_tiles[step][:].bitcast(F32)[:, i, 256 * gl + u : 256 * (gl + 1) : 2]
 
         def transposes(step):
-            banks = []
-            for gl in range(2):
-                for ip in range(2):
-                    tp = psum_t.tile([P, 2, 2, P], F32, name="tp", tag="tp")
-                    for il in range(2):
-                        for u in range(2):
-                            nc.tensor.transpose(tp[:, il, u, :], words(step, gl, 2 * ip + il, u), ident[:])
-                    banks.append(tp)
-            return banks
+            banks = {}
+            order = [(gl, ip) for gl in range(2) for ip in range(2)]
+            if 2 <= step <= SPLIT_LAST:
+                order = [(gl, ip) for ip in range(2) for gl in range(2)]
+            for gl, ip in order:
+                tp = psum_t.tile([P, 2, 2, P], F32, name="tp", tag="tp")
+                for il in range(2):
+                    for u in range(2):
+                        nc.tensor.transpose(tp[:, il, u, :], words(step, gl, 2 * ip + il, u), ident[:])
+                banks[(gl, ip)] = tp
+            return order, banks
 
         def copies(step, banks):
             gt = stage.tile([P, 4096], BF16, name="grouped", tag="grouped", align_bytes=64)
             gw = gt[:].bitcast(F32).rearrange("p (g i r u) -> p g i r u", g=2, i=4, u=2)
-            for gl in range(2):
-                for ip in range(2):
-                    src = banks[2 * gl + ip][:].rearrange("p i u r -> p i r u")
-                    if step <= LAG and ip == 1 and gl == 1:
+            order, tiles = banks
+            for gl, ip in order:
+                if True:
+                    src = tiles[(gl, ip)][:].rearrange("p i u r -> p i r u")
+                    if step <= LAG + 2 and ip == 1 and gl == 1:
                         nc.vector.tensor_copy(out=gw[:, gl, 2 * ip : 2 * ip + 2], in_=src)
                     else:
                         nc.scalar.copy(out=gw[:, gl, 2 * ip : 2 * ip + 2], in_=src)
@@ -224,9 +233,9 @@ def tile_efficientattention_pa_kernel(tc, x, Wq, Wk, Wv, out_0, out_1, out_2):
                 o_tiles[n] = ot
             if n == GROUPS - 1:
                 nc.scalar.copy(out=o_tiles[n][:, :, 2 * ap, :], in_=accs[0][:].rearrange("p (h d) -> p h d", h=4))
-                nc.sync.dma_start(out=out_view(n)[:, :, 2 * ap, :], in_=o_tiles[n][:, :, 2 * ap, :])
-                nc.vector.tensor_copy(out=o_tiles[n][:, :, 2 * ap + 1, :], in_=accs[1][:].rearrange("p (h d) -> p h d", h=4))
-                nc.sync.dma_start(out=out_view(n)[:, :, 2 * ap + 1, :], in_=o_tiles[n][:, :, 2 * ap + 1, :])
+                nc.scalar.dma_start(out=out_view(n)[:, :, 2 * ap, :], in_=o_tiles[n][:, :, 2 * ap, :])
+                nc.scalar.copy(out=o_tiles[n][:, :, 2 * ap + 1, :], in_=accs[1][:].rearrange("p (h d) -> p h d", h=4))
+                nc.scalar.dma_start(out=out_view(n)[:, :, 2 * ap + 1, :], in_=o_tiles[n][:, :, 2 * ap + 1, :])
                 return
             pr = work.tile([P, 2, 2, 512], F32, name="prod", tag="prod", bufs=3)
             prods[mm] = pr
@@ -239,8 +248,6 @@ def tile_efficientattention_pa_kernel(tc, x, Wq, Wk, Wv, out_0, out_1, out_2):
                     in1=accs[al][:].rearrange("p (h d) -> p h d", d=HD).unsqueeze(1).to_broadcast([P, 2, 4, HD]),
                     op=ALU.mult,
                 )
-                if last_rope:
-                    continue
                 if al == 0:
                     add(nc.gpsimd, mm, 0, 1, 0)
                 else:
@@ -265,8 +272,6 @@ def tile_efficientattention_pa_kernel(tc, x, Wq, Wk, Wv, out_0, out_1, out_2):
                 return
             last_rope = n == GROUPS - 2
             if last_rope:
-                for t in range(2):
-                    add(nc.vector, mm, 0, 2, t)
                 nc.sync.dma_start(
                     out=out_view(n)[:, :, 2 * ap : 2 * ap + 2, :].rearrange("r h a d -> r h (a d)"),
                     in_=o_tiles[n][:, :, 2 * ap : 2 * ap + 2, :].rearrange("p h a d -> p h (a d)"),

@@ -26,6 +26,8 @@ RAW_BUFS = 8
 R0 = 6
 R_TILES = 3
 SPLIT_LAST = 5
+X_STEPS = [0, 1]
+MM_EARLY = {4: 0, 5: 1}
 HALF = 64
 RATIO = 10000.0 ** (-1.0 / 64.0)
 TWO_PI = 2.0 * math.pi
@@ -48,19 +50,25 @@ def tile_efficientattention_pa_kernel(tc, x, Wq, Wk, Wv, out_0, out_1, out_2):
         xv = x.flatten_outer_dims().rearrange("(r a) k -> r a k", a=4)
         raw_tiles = {}
 
+        def w_of(step):
+            w = step - 1 if step < X_STEPS[1] else step - 2
+            return w // 2, w % 2
+
         def load(step):
+            if step in X_STEPS:
+                t = raw.tile([P, 2, 2048], BF16, name="raw_t", tag="raw_t")
+                raw_tiles[step] = t
+                a0 = 2 * X_STEPS.index(step)
+                if step == 0:
+                    nc.sync.dma_start(out=t[:, 0, 0:1024], in_=xv[:, a0, 0:1024])
+                    nc.sync.dma_start(out=t[:, 0, 1024:2048], in_=xv[:, a0, 1024:2048])
+                else:
+                    nc.sync.dma_start(out=t[:, 0, :], in_=xv[:, a0, :])
+                nc.sync.dma_start(out=t[:, 1, :], in_=xv[:, a0 + 1, :])
+                return
             t = raw.tile([P, 4, 1024], BF16, name="raw_t", tag="raw_t")
             raw_tiles[step] = t
-            if step == 0:
-                nc.sync.dma_start(out=t[:, 0:2, 0:512], in_=xv[:, 0:2, 0:512])
-                nc.sync.dma_start(out=t[:, 2:4, 0:512], in_=xv[:, 2:4, 0:512])
-                nc.sync.dma_start(out=t[:, :, 512:1024], in_=xv[:, :, 512:1024])
-                return
-            if step == 1:
-                nc.sync.dma_start(out=t[:, :, 0:512], in_=xv[:, :, 1024:1536])
-                nc.sync.dma_start(out=t[:, :, 512:1024], in_=xv[:, :, 1536:2048])
-                return
-            n, gp = (step - 2) // 2, (step - 2) % 2
+            n, gp = w_of(step)
             if n < 4:
                 src = Wq[512 * n : 512 * (n + 1), :]
             elif n == 4:
@@ -132,14 +140,15 @@ def tile_efficientattention_pa_kernel(tc, x, Wq, Wk, Wv, out_0, out_1, out_2):
             for t in range(2):
                 nc.scalar.activation(out=cs_tab[:, :, 0, t, :], in_=absr[:], func=ACT.Sin, scale=-1.0, bias=math.pi / 2.0)
 
-        x_codes = const.tile([P, PASSES, 512], U32, name="x_codes", tag="x_codes", align_bytes=64)
-        x_scales = const.tile([P, PASSES, 512], U8, name="x_scales", tag="x_scales", align_bytes=64)
+        x_codes = const.tile([P, 2, PASSES, 256], U32, name="x_codes", tag="x_codes", align_bytes=64)
+        x_scales = const.tile([P, 2, PASSES, 256], U8, name="x_scales", tag="x_scales", align_bytes=64)
         w_codes = {}
         w_scales = {}
         o_tiles = {}
         prods = {}
 
         ro_tiles = {}
+        rg_tiles = {}
 
         def reorder(step):
             if step < R0 or step >= N_T:
@@ -150,44 +159,69 @@ def tile_efficientattention_pa_kernel(tc, x, Wq, Wk, Wv, out_0, out_1, out_2):
                 out=ro[:].rearrange("p i (g u m) -> p (i g) u m", g=2, u=2),
                 in_=raw_tiles[step][:].bitcast(F32)[:, 0:R_TILES, :].rearrange("p i (g m u) -> p (i g) u m", g=2, u=2),
             )
+            rg = stage.tile([P, 1024], BF16, name="rg", tag="rg")
+            rg_tiles[step] = rg
+            for g in range(2):
+                nc.gpsimd.tensor_scalar(
+                    out=rg[:, 512 * g : 512 * (g + 1)].rearrange("p (u m e) -> p u m e", u=2, e=2),
+                    in0=raw_tiles[step][:, 3, 512 * g : 512 * (g + 1)].rearrange("p (m u e) -> p u m e", u=2, e=2),
+                    scalar1=1.0,
+                    scalar2=0.0,
+                    op0=ALU.mult,
+                    op1=ALU.add,
+                )
 
         def words(step, gl, i, u):
             if step >= R0 and i < R_TILES:
                 return ro_tiles[step][:, i, 256 * gl + 128 * u : 256 * gl + 128 * (u + 1)]
+            if step >= R0:
+                return rg_tiles[step][:].bitcast(F32)[:, 256 * gl + 128 * u : 256 * gl + 128 * (u + 1)]
             return raw_tiles[step][:].bitcast(F32)[:, i, 256 * gl + u : 256 * (gl + 1) : 2]
 
         def transposes(step):
             banks = {}
             order = [(gl, ip) for gl in range(2) for ip in range(2)]
-            if 2 <= step <= SPLIT_LAST:
+            if step <= SPLIT_LAST:
                 order = [(gl, ip) for ip in range(2) for gl in range(2)]
             for gl, ip in order:
                 tp = psum_t.tile([P, 2, 2, P], F32, name="tp", tag="tp")
                 for il in range(2):
                     for u in range(2):
-                        nc.tensor.transpose(tp[:, il, u, :], words(step, gl, 2 * ip + il, u), ident[:])
+                        if step in X_STEPS:
+                            g = 2 * gl + il
+                            src = raw_tiles[step][:].bitcast(F32)[:, ip, 256 * g + u : 256 * (g + 1) : 2]
+                        else:
+                            src = words(step, gl, 2 * ip + il, u)
+                        nc.tensor.transpose(tp[:, il, u, :], src, ident[:])
                 banks[(gl, ip)] = tp
             return order, banks
 
         def copies(step, banks):
             gt = stage.tile([P, 4096], BF16, name="grouped", tag="grouped", align_bytes=64)
             gw = gt[:].bitcast(F32).rearrange("p (g i r u) -> p g i r u", g=2, i=4, u=2)
+            gx = gt[:].bitcast(F32).rearrange("p (g i r u) -> p g i r u", g=4, i=2, u=2)
             order, tiles = banks
             for gl, ip in order:
-                if True:
-                    src = tiles[(gl, ip)][:].rearrange("p i u r -> p i r u")
-                    if step <= LAG + 2 and ip == 1 and gl == 1:
-                        nc.vector.tensor_copy(out=gw[:, gl, 2 * ip : 2 * ip + 2], in_=src)
-                    else:
-                        nc.scalar.copy(out=gw[:, gl, 2 * ip : 2 * ip + 2], in_=src)
+                src = tiles[(gl, ip)][:].rearrange("p i u r -> p i r u")
+                dst = gx[:, 2 * gl : 2 * gl + 2, ip] if step in X_STEPS else gw[:, gl, 2 * ip : 2 * ip + 2]
+                if step <= LAG + 2 and ip == 1 and gl == 1:
+                    nc.vector.tensor_copy(out=dst, in_=src)
+                else:
+                    nc.scalar.copy(out=dst, in_=src)
             return gt
 
         def quantize(step, grouped):
-            if step < 2:
-                codes, scales, g0 = x_codes, x_scales, 2 * step
-            else:
-                n = (step - 2) // 2
-                g0 = 2 * ((step - 2) % 2)
+            if step in X_STEPS:
+                half = X_STEPS.index(step)
+                nc.vector.quantize_mx(
+                    out=x_codes[:, half, :, :].rearrange("p g c -> p (g c)").bitcast(E5X4),
+                    scales=x_scales[:, half, :, :].rearrange("p g c -> p (g c)"),
+                    in_=grouped[:],
+                )
+                return
+            if True:
+                n, gp = w_of(step)
+                g0 = 2 * gp
                 if g0 == 0:
                     wc = wq_pool.tile([P, PASSES, 512], U32, name="w_codes", tag="w_codes", align_bytes=64)
                     ws = wq_pool.tile([P, PASSES, 512], U8, name="w_scales", tag="w_scales", align_bytes=64)
@@ -209,8 +243,8 @@ def tile_efficientattention_pa_kernel(tc, x, Wq, Wk, Wv, out_0, out_1, out_2):
                 for g in range(PASSES):
                     nc.tensor.matmul_mx(
                         out=acc[:],
-                        lhsT=x_codes[:, g, P * a : P * (a + 1)].bitcast(E5X4),
-                        lhsT_scale=x_scales[:, g, P * a : P * (a + 1)],
+                        lhsT=x_codes[:, ap, g, P * al : P * (al + 1)].bitcast(E5X4),
+                        lhsT_scale=x_scales[:, ap, g, P * al : P * (al + 1)],
                         rhs=w_codes[n][:, g, :].bitcast(E5X4),
                         rhs_scale=w_scales[n][:, g, :],
                         start=(g == 0),
@@ -283,11 +317,14 @@ def tile_efficientattention_pa_kernel(tc, x, Wq, Wk, Wv, out_0, out_1, out_2):
                 )
 
         for step in range(N_MM + LAG):
-            mm = step - LAG
+            mm = step - LAG if step >= LAG + 2 else MM_EARLY.get(step, -1)
             if step < N_T:
                 banks = transposes(step)
                 grouped = copies(step, banks)
-                reorder(step + 2)
+                if step == R0 - 1:
+                    reorder(R0)
+                if step + 2 > R0:
+                    reorder(step + 2)
                 if step + RAW_BUFS < N_T:
                     load(step + RAW_BUFS)
             if step == 1:

@@ -148,7 +148,6 @@ def tile_efficientattention_pa_kernel(tc, x, Wq, Wk, Wv, out_0, out_1, out_2):
         prods = {}
 
         ro_tiles = {}
-        rg_tiles = {}
 
         def reorder(step):
             if step < R0 or step >= N_T:
@@ -159,23 +158,10 @@ def tile_efficientattention_pa_kernel(tc, x, Wq, Wk, Wv, out_0, out_1, out_2):
                 out=ro[:].rearrange("p i (g u m) -> p (i g) u m", g=2, u=2),
                 in_=raw_tiles[step][:].bitcast(F32)[:, 0:R_TILES, :].rearrange("p i (g m u) -> p (i g) u m", g=2, u=2),
             )
-            rg = stage.tile([P, 1024], BF16, name="rg", tag="rg")
-            rg_tiles[step] = rg
-            for g in range(2):
-                nc.gpsimd.tensor_scalar(
-                    out=rg[:, 512 * g : 512 * (g + 1)].rearrange("p (u m e) -> p u m e", u=2, e=2),
-                    in0=raw_tiles[step][:, 3, 512 * g : 512 * (g + 1)].rearrange("p (m u e) -> p u m e", u=2, e=2),
-                    scalar1=1.0,
-                    scalar2=0.0,
-                    op0=ALU.mult,
-                    op1=ALU.add,
-                )
 
         def words(step, gl, i, u):
             if step >= R0 and i < R_TILES:
                 return ro_tiles[step][:, i, 256 * gl + 128 * u : 256 * gl + 128 * (u + 1)]
-            if step >= R0:
-                return rg_tiles[step][:].bitcast(F32)[:, 256 * gl + 128 * u : 256 * gl + 128 * (u + 1)]
             return raw_tiles[step][:].bitcast(F32)[:, i, 256 * gl + u : 256 * (gl + 1) : 2]
 
         def transposes(step):

@@ -26,6 +26,7 @@ RAW_BUFS = 8
 R0 = 6
 R_TILES = 3
 SPLIT_LAST = 5
+N_WARM = 6
 X_STEPS = [0, 1]
 MM_EARLY = {4: 0, 5: 1}
 HALF = 64
@@ -84,6 +85,12 @@ def tile_efficientattention_pa_kernel(tc, x, Wq, Wk, Wv, out_0, out_1, out_2):
 
         for step in range(RAW_BUFS):
             load(step)
+
+        wz = const.tile([P, 512], BF16, name="wz", tag="wz")
+        nc.vector.memset(wz[:], 0.0)
+        for w in range(N_WARM):
+            wacc = psum_m.tile([P, 512], F32, name="acc", tag="acc")
+            nc.tensor.matmul(out=wacc[:], lhsT=wz[:, 0:P], rhs=wz[:], start=True, stop=True)
 
         ident = const.tile([P, P], F32, name="ident", tag="ident")
         make_identity(nc, ident[:])

@@ -26,6 +26,7 @@ RAW_BUFS = 8
 R0 = 6
 R_TILES = 3
 SPLIT_LAST = 5
+V_ADDS = [9]
 N_WARM = 6
 X_STEPS = [0, 1]
 MM_EARLY = {4: 0, 5: 1}
@@ -275,7 +276,11 @@ def tile_efficientattention_pa_kernel(tc, x, Wq, Wk, Wv, out_0, out_1, out_2):
                     in1=accs[al][:].rearrange("p (h d) -> p h d", d=HD).unsqueeze(1).to_broadcast([P, 2, 4, HD]),
                     op=ALU.mult,
                 )
-                if al == 0:
+                if mm in V_ADDS:
+                    if al == 1:
+                        for t in range(2):
+                            add(nc.vector, mm, 0, 2, t)
+                elif al == 0:
                     add(nc.gpsimd, mm, 0, 1, 0)
                 else:
                     add(nc.vector, mm, 0, 1, 1)

@@ -23,8 +23,20 @@ N_T = 2 + 2 * GROUPS
 N_MM = 2 * GROUPS
 LAG = 4
 RAW_BUFS = 8
-R0 = 6
+R0 = 5
 R_TILES = 3
+R_FULL = 12
+SORT_PLAN = {
+    4: [(5, 0, 3)],
+    5: [(6, 0, 3), (7, 0, 3)],
+    6: [(8, 0, 3)],
+    7: [(9, 0, 3)],
+    8: [(10, 0, 3)],
+    9: [(11, 0, 3)],
+    10: [(12, 0, 3)],
+    11: [(12, 3, 4), (13, 0, 2)],
+    12: [(13, 2, 4)],
+}
 SPLIT_LAST = 5
 V_ADDS = [9]
 N_WARM = 6
@@ -157,18 +169,17 @@ def tile_efficientattention_pa_kernel(tc, x, Wq, Wk, Wv, out_0, out_1, out_2):
 
         ro_tiles = {}
 
-        def reorder(step):
-            if step < R0 or step >= N_T:
-                return
-            ro = stage.tile([P, R_TILES, 512], F32, name="ro", tag="ro")
-            ro_tiles[step] = ro
+        def reorder(step, i0, i1):
+            if step not in ro_tiles:
+                ro = stage.tile([P, 4, 512], F32, name="ro", tag="ro")
+                ro_tiles[step] = ro
             nc.scalar.copy(
-                out=ro[:].rearrange("p i (g u m) -> p (i g) u m", g=2, u=2),
-                in_=raw_tiles[step][:].bitcast(F32)[:, 0:R_TILES, :].rearrange("p i (g m u) -> p (i g) u m", g=2, u=2),
+                out=ro_tiles[step][:, i0:i1, :].rearrange("p i (g u m) -> p (i g) u m", g=2, u=2),
+                in_=raw_tiles[step][:].bitcast(F32)[:, i0:i1, :].rearrange("p i (g m u) -> p (i g) u m", g=2, u=2),
             )
 
         def words(step, gl, i, u):
-            if step >= R0 and i < R_TILES:
+            if step >= R_FULL or (step >= R0 and i < R_TILES):
                 return ro_tiles[step][:, i, 256 * gl + 128 * u : 256 * gl + 128 * (u + 1)]
             return raw_tiles[step][:].bitcast(F32)[:, i, 256 * gl + u : 256 * (gl + 1) : 2]
 
@@ -319,10 +330,8 @@ def tile_efficientattention_pa_kernel(tc, x, Wq, Wk, Wv, out_0, out_1, out_2):
             if step < N_T:
                 banks = transposes(step)
                 grouped = copies(step, banks)
-                if step == R0 - 1:
-                    reorder(R0)
-                if step + 2 > R0:
-                    reorder(step + 2)
+                for s_step, i0, i1 in SORT_PLAN.get(step, []):
+                    reorder(s_step, i0, i1)
                 if step + RAW_BUFS < N_T:
                     load(step + RAW_BUFS)
             if step == 1:

@@ -27,7 +27,7 @@ R0 = 5
 R_TILES = 3
 R_FULL = 12
 SORT_PLAN = {
-    4: [(5, 0, 3)],
+    4: [(5, 0, 2), (5, 2, 4)],
     5: [(6, 0, 3), (7, 0, 3)],
     6: [(8, 0, 3)],
     7: [(9, 0, 3)],
@@ -179,7 +179,7 @@ def tile_efficientattention_pa_kernel(tc, x, Wq, Wk, Wv, out_0, out_1, out_2):
             )
 
         def words(step, gl, i, u):
-            if step >= R_FULL or (step >= R0 and i < R_TILES):
+            if step >= R_FULL or step == R0 or (step >= R0 and i < R_TILES):
                 return ro_tiles[step][:, i, 256 * gl + 128 * u : 256 * gl + 128 * (u + 1)]
             return raw_tiles[step][:].bitcast(F32)[:, i, 256 * gl + u : 256 * (gl + 1) : 2]
 

@@ -171,16 +171,16 @@ def tile_efficientattention_pa_kernel(tc, x, Wq, Wk, Wv, out_0, out_1, out_2):
 
         def reorder(step, i0, i1):
             if step not in ro_tiles:
-                ro = stage.tile([P, 4, 512], F32, name="ro", tag="ro")
+                ro = stage.tile([P, 2, 8, P], F32, name="ro", tag="ro")
                 ro_tiles[step] = ro
             nc.scalar.copy(
-                out=ro_tiles[step][:, i0:i1, :].rearrange("p i (g u m) -> p (i g) u m", g=2, u=2),
-                in_=raw_tiles[step][:].bitcast(F32)[:, i0:i1, :].rearrange("p i (g m u) -> p (i g) u m", g=2, u=2),
+                out=ro_tiles[step][:, :, 2 * i0 : 2 * i1, :].rearrange("p u b (c j) -> p (b c) u j", j=4),
+                in_=raw_tiles[step][:].bitcast(F32)[:, i0:i1, :].rearrange("p i (c j u) -> p (i c) u j", j=4, u=2),
             )
 
         def words(step, gl, i, u):
             if step >= R_FULL or step == R0 or (step >= R0 and i < R_TILES):
-                return ro_tiles[step][:, i, 256 * gl + 128 * u : 256 * gl + 128 * (u + 1)]
+                return ro_tiles[step][:, u, 2 * i + gl, :]
             return raw_tiles[step][:].bitcast(F32)[:, i, 256 * gl + u : 256 * (gl + 1) : 2]
 
         def transposes(step):

@@ -39,6 +39,7 @@ SORT_PLAN = {
 }
 SPLIT_LAST = 5
 V_ADDS = [9]
+G_HEADS = 3
 N_WARM = 6
 X_STEPS = [0, 1]
 MM_EARLY = {4: 0, 5: 1}
@@ -291,12 +292,32 @@ def tile_efficientattention_pa_kernel(tc, x, Wq, Wk, Wv, out_0, out_1, out_2):
                     if al == 1:
                         for t in range(2):
                             add(nc.vector, mm, 0, 2, t)
-                elif al == 0:
-                    add(nc.gpsimd, mm, 0, 1, 0)
                 else:
-                    add(nc.vector, mm, 0, 1, 1)
-                    add(nc.gpsimd, mm, 1, 2, 0)
-                    add(nc.gpsimd, mm, 1, 2, 1)
+                    head_add(nc.gpsimd, mm, al, al + 1, 0, G_HEADS)
+                if al == 0 and mm >= 1:
+                    head_add(nc.vector, mm - 1, 0, 2, G_HEADS, 4)
+                    sums(mm - 1)
+            if mm in V_ADDS:
+                sums(mm)
+
+        def head_add(eng, mm, al0, al1, h0, h1):
+            n, ap = mm // 2, mm % 2
+            prv = prods[mm][:].rearrange("p a c (h t j) -> p a c h t j", h=4, t=2)
+            ov = o_tiles[n][:].rearrange("p h a (t j) -> p a h t j", t=2)
+            if al1 - al0 == 1:
+                eng.tensor_tensor(
+                    out=ov[:, 2 * ap + al0, h0:h1, :, :],
+                    in0=prv[:, al0, 0, h0:h1, :, :],
+                    in1=prv[:, al0, 1, h0:h1, ::-1, :],
+                    op=ALU.add,
+                )
+            else:
+                eng.tensor_tensor(
+                    out=ov[:, 2 * ap + al0 : 2 * ap + al1, h0, :, :],
+                    in0=prv[:, al0:al1, 0, h0, :, :],
+                    in1=prv[:, al0:al1, 1, h0, ::-1, :],
+                    op=ALU.add,
+                )
 
         def add(eng, mm, al0, al1, t):
             n, ap = mm // 2, mm % 2
@@ -341,4 +362,3 @@ def tile_efficientattention_pa_kernel(tc, x, Wq, Wk, Wv, out_0, out_1, out_2):
             if mm >= 0:
                 accs = matmuls(mm)
                 products(mm, accs)
-                sums(mm)

@@ -161,8 +161,10 @@ def tile_efficientattention_pa_kernel(tc, x, Wq, Wk, Wv, out_0, out_1, out_2):
             for t in range(2):
                 nc.scalar.activation(out=cs_tab[:, :, 0, t, :], in_=absr[:], func=ACT.Sin, scale=-1.0, bias=math.pi / 2.0)
 
-        x_codes = const.tile([P, 2, PASSES, 256], U32, name="x_codes", tag="x_codes", align_bytes=64)
-        x_scales = const.tile([P, 2, PASSES, 256], U8, name="x_scales", tag="x_scales", align_bytes=64)
+        xc_tile = const.tile([P, 32 + 2048], U32, name="x_codes", tag="x_codes", align_bytes=256)
+        xs_tile = const.tile([P, 192 + 2048], U8, name="x_scales", tag="x_scales", align_bytes=256)
+        x_codes = xc_tile[:, 32:].rearrange("p (a g c) -> p a g c", a=2, g=PASSES)
+        x_scales = xs_tile[:, 192:].rearrange("p (a g c) -> p a g c", a=2, g=PASSES)
         w_codes = {}
         w_scales = {}
         o_tiles = {}
@@ -229,10 +231,10 @@ def tile_efficientattention_pa_kernel(tc, x, Wq, Wk, Wv, out_0, out_1, out_2):
                 n, gp = w_of(step)
                 g0 = 2 * gp
                 if g0 == 0:
-                    wc = wq_pool.tile([P, PASSES, 512], U32, name="w_codes", tag="w_codes", align_bytes=64)
-                    ws = wq_pool.tile([P, PASSES, 512], U8, name="w_scales", tag="w_scales", align_bytes=64)
+                    wc = wq_pool.tile([P, PASSES, 512], U32, name="w_codes", tag="w_codes", align_bytes=256)
+                    ws = wq_pool.tile([P, 64 + PASSES * 512], U8, name="w_scales", tag="w_scales", align_bytes=256)
                     w_codes[n] = wc
-                    w_scales[n] = ws
+                    w_scales[n] = ws[:, 64:].rearrange("p (g c) -> p g c", g=PASSES)
                 codes, scales = w_codes[n], w_scales[n]
             nc.vector.quantize_mx(
                 out=codes[:, g0 : g0 + 2, :].rearrange("p g c -> p (g c)").bitcast(E5X4),

@@ -34,9 +34,9 @@ SORT_PLAN = {
     8: [(10, 0, 3)],
     9: [(11, 0, 3)],
     10: [(12, 0, 3)],
-    11: [(12, 3, 4), (13, 0, 2)],
-    12: [(13, 2, 4)],
+    11: [(12, 3, 4), (13, 0, 2), (13, 2, 4)],
 }
+PAIR_FROM = 6
 SPLIT_LAST = 5
 V_ADDS = [9]
 G_HEADS = 3
@@ -59,8 +59,7 @@ def tile_efficientattention_pa_kernel(tc, x, Wq, Wk, Wv, out_0, out_1, out_2):
         stage = ctx.enter_context(tc.tile_pool(name="stage", bufs=3))
         wq_pool = ctx.enter_context(tc.tile_pool(name="wq_pool", bufs=3))
         work = ctx.enter_context(tc.tile_pool(name="work", bufs=2))
-        psum_t = ctx.enter_context(tc.psum_pool(name="psum_t", bufs=4))
-        psum_m = ctx.enter_context(tc.psum_pool(name="psum_m", bufs=4))
+        psum = ctx.enter_context(tc.psum_pool(name="psum", bufs=8))
 
         xv = x.flatten_outer_dims().rearrange("(r a) k -> r a k", a=4)
         raw_tiles = {}
@@ -103,7 +102,7 @@ def tile_efficientattention_pa_kernel(tc, x, Wq, Wk, Wv, out_0, out_1, out_2):
         wz = const.tile([P, 512], BF16, name="wz", tag="wz")
         nc.vector.memset(wz[:], 0.0)
         for w in range(N_WARM):
-            wacc = psum_m.tile([P, 512], F32, name="acc", tag="acc")
+            wacc = psum.tile([P, 512], F32, name="bank", tag="bank")
             nc.tensor.matmul(out=wacc[:], lhsT=wz[:, 0:P], rhs=wz[:], start=True, stop=True)
 
         ident = const.tile([P, P], F32, name="ident", tag="ident")
@@ -192,7 +191,7 @@ def tile_efficientattention_pa_kernel(tc, x, Wq, Wk, Wv, out_0, out_1, out_2):
             if step <= SPLIT_LAST:
                 order = [(gl, ip) for ip in range(2) for gl in range(2)]
             for gl, ip in order:
-                tp = psum_t.tile([P, 2, 2, P], F32, name="tp", tag="tp")
+                tp = psum.tile([P, 2, 2, P], F32, name="bank", tag="bank")
                 for il in range(2):
                     for u in range(2):
                         if step in X_STEPS:
@@ -247,7 +246,7 @@ def tile_efficientattention_pa_kernel(tc, x, Wq, Wk, Wv, out_0, out_1, out_2):
             accs = []
             for al in range(2):
                 a = 2 * ap + al
-                acc = psum_m.tile([P, 512], F32, name="acc", tag="acc")
+                acc = psum.tile([P, 512], F32, name="bank", tag="bank")
                 for g in range(PASSES):
                     nc.tensor.matmul_mx(
                         out=acc[:],
@@ -348,19 +347,30 @@ def tile_efficientattention_pa_kernel(tc, x, Wq, Wk, Wv, out_0, out_1, out_2):
                     in_=o_tiles[n][:].rearrange("p h a d -> p h (a d)"),
                 )
 
-        for step in range(N_MM + LAG):
-            mm = step - LAG if step >= LAG + 2 else MM_EARLY.get(step, -1)
-            if step < N_T:
-                banks = transposes(step)
-                grouped = copies(step, banks)
-                for s_step, i0, i1 in SORT_PLAN.get(step, []):
-                    reorder(s_step, i0, i1)
-                if step + RAW_BUFS < N_T:
-                    load(step + RAW_BUFS)
-            if step == 1:
-                finish_tables()
-            if step < N_T:
-                quantize(step, grouped)
-            if mm >= 0:
-                accs = matmuls(mm)
-                products(mm, accs)
+        runs = [[s] for s in range(PAIR_FROM)]
+        runs.extend([[s, s + 1] for s in range(PAIR_FROM, N_T, 2)])
+        runs.extend([[s] for s in range(N_T, N_MM + LAG)])
+        for run in runs:
+            banks = {}
+            grouped = {}
+            for step in run:
+                if step < N_T:
+                    banks[step] = transposes(step)
+            for step in run:
+                if step < N_T:
+                    grouped[step] = copies(step, banks[step])
+            for step in run:
+                if step < N_T:
+                    for s_step, i0, i1 in SORT_PLAN.get(step, []):
+                        reorder(s_step, i0, i1)
+                    if step + RAW_BUFS < N_T:
+                        load(step + RAW_BUFS)
+            for step in run:
+                mm = step - LAG if step >= LAG + 2 else MM_EARLY.get(step, -1)
+                if step == 1:
+                    finish_tables()
+                if step < N_T:
+                    quantize(step, grouped[step])
+                if mm >= 0:
+                    accs = matmuls(mm)
+                    products(mm, accs)

@@ -25,7 +25,7 @@ LAG = 4
 RAW_BUFS = 8
 R0 = 5
 R_TILES = 3
-R_FULL = 12
+R_FULL = 8
 SORT_PLAN = {
     4: [(5, 0, 2), (5, 2, 4)],
     5: [(6, 0, 3), (7, 0, 3)],
@@ -34,9 +34,10 @@ SORT_PLAN = {
     8: [(10, 0, 3)],
     9: [(11, 0, 3)],
     10: [(12, 0, 3)],
-    11: [(12, 3, 4), (13, 0, 2), (13, 2, 4)],
+    11: [(13, 0, 3)],
 }
-PAIR_FROM = 6
+V_SORT = {6: [8, 9], 8: [10, 11], 10: [12, 13]}
+PHASES = [([0], []), ([1], []), ([2], []), ([3], []), ([4], [0]), ([5], [1]), ([6, 7], [2, 3]), ([8, 9], [4, 5]), ([10, 11], [6, 7]), ([12, 13], [8, 9]), ([], [10]), ([], [11])]
 SPLIT_LAST = 5
 V_ADDS = [9]
 G_HEADS = 3
@@ -171,11 +172,12 @@ def tile_efficientattention_pa_kernel(tc, x, Wq, Wk, Wv, out_0, out_1, out_2):
 
         ro_tiles = {}
 
-        def reorder(step, i0, i1):
+        def reorder(step, i0, i1, on_vector=False):
             if step not in ro_tiles:
                 ro = stage.tile([P, 2, 8, P], F32, name="ro", tag="ro")
                 ro_tiles[step] = ro
-            nc.scalar.copy(
+            copy = nc.vector.tensor_copy if on_vector else nc.scalar.copy
+            copy(
                 out=ro_tiles[step][:, :, 2 * i0 : 2 * i1, :].rearrange("p u b (c j) -> p (b c) u j", j=4),
                 in_=raw_tiles[step][:].bitcast(F32)[:, i0:i1, :].rearrange("p i (c j u) -> p (i c) u j", j=4, u=2),
             )
@@ -347,30 +349,25 @@ def tile_efficientattention_pa_kernel(tc, x, Wq, Wk, Wv, out_0, out_1, out_2):
                     in_=o_tiles[n][:].rearrange("p h a d -> p h (a d)"),
                 )
 
-        runs = [[s] for s in range(PAIR_FROM)]
-        runs.extend([[s, s + 1] for s in range(PAIR_FROM, N_T, 2)])
-        runs.extend([[s] for s in range(N_T, N_MM + LAG)])
-        for run in runs:
+        for t_steps, units in PHASES:
             banks = {}
             grouped = {}
-            for step in run:
-                if step < N_T:
-                    banks[step] = transposes(step)
-            for step in run:
-                if step < N_T:
-                    grouped[step] = copies(step, banks[step])
-            for step in run:
-                if step < N_T:
-                    for s_step, i0, i1 in SORT_PLAN.get(step, []):
-                        reorder(s_step, i0, i1)
-                    if step + RAW_BUFS < N_T:
-                        load(step + RAW_BUFS)
-            for step in run:
-                mm = step - LAG if step >= LAG + 2 else MM_EARLY.get(step, -1)
-                if step == 1:
-                    finish_tables()
-                if step < N_T:
-                    quantize(step, grouped[step])
-                if mm >= 0:
-                    accs = matmuls(mm)
-                    products(mm, accs)
+            for step in t_steps:
+                banks[step] = transposes(step)
+            for step in t_steps:
+                grouped[step] = copies(step, banks[step])
+            for step in t_steps:
+                for s_step, i0, i1 in SORT_PLAN.get(step, []):
+                    reorder(s_step, i0, i1)
+                if step + RAW_BUFS < N_T:
+                    load(step + RAW_BUFS)
+            for slot in range(max(len(t_steps), len(units))):
+                if slot < len(t_steps):
+                    if t_steps[slot] == 1:
+                        finish_tables()
+                    quantize(t_steps[slot], grouped[t_steps[slot]])
+                    for s_step in V_SORT.get(t_steps[slot], []):
+                        reorder(s_step, 3, 4, on_vector=True)
+                if slot < len(units):
+                    accs = matmuls(units[slot])
+                    products(units[slot], accs)

@@ -27,8 +27,8 @@ R0 = 5
 R_TILES = 3
 R_FULL = 8
 SORT_PLAN = {
-    4: [(5, 0, 2), (5, 2, 4)],
-    5: [(6, 0, 3), (7, 0, 3)],
+    4: [(5, 0, 2), (5, 2, 3)],
+    5: [(6, 0, 2), (7, 0, 2)],
     6: [(8, 0, 3)],
     7: [(9, 0, 3)],
     8: [(10, 0, 3)],
@@ -36,7 +36,9 @@ SORT_PLAN = {
     10: [(12, 0, 3)],
     11: [(13, 0, 3)],
 }
-V_SORT = {6: [8, 9], 8: [10, 11], 10: [12, 13]}
+V_SORT = {6: [8], 8: [10], 10: [12]}
+SORTED = {5: 3, 6: 2, 7: 2, 8: 4, 9: 3, 10: 4, 11: 3, 12: 4, 13: 3}
+V_BANK_LAST = 3
 PHASES = [([0], []), ([1], []), ([2], []), ([3], []), ([4], [0]), ([5], [1]), ([6, 7], [2, 3]), ([8, 9], [4, 5]), ([10, 11], [6, 7]), ([12, 13], [8, 9]), ([], [10]), ([], [11])]
 SPLIT_LAST = 5
 V_ADDS = [9]
@@ -183,7 +185,7 @@ def tile_efficientattention_pa_kernel(tc, x, Wq, Wk, Wv, out_0, out_1, out_2):
             )
 
         def words(step, gl, i, u):
-            if step >= R_FULL or step == R0 or (step >= R0 and i < R_TILES):
+            if i < SORTED.get(step, 0):
                 return ro_tiles[step][:, u, 2 * i + gl, :]
             return raw_tiles[step][:].bitcast(F32)[:, i, 256 * gl + u : 256 * (gl + 1) : 2]
 
@@ -213,7 +215,7 @@ def tile_efficientattention_pa_kernel(tc, x, Wq, Wk, Wv, out_0, out_1, out_2):
             for gl, ip in order:
                 src = tiles[(gl, ip)][:].rearrange("p i u r -> p i r u")
                 dst = gx[:, 2 * gl : 2 * gl + 2, ip] if step in X_STEPS else gw[:, gl, 2 * ip : 2 * ip + 2]
-                if step <= LAG + 2 and ip == 1 and gl == 1:
+                if step <= V_BANK_LAST and ip == 1 and gl == 1:
                     nc.vector.tensor_copy(out=dst, in_=src)
                 else:
                     nc.scalar.copy(out=dst, in_=src)

@@ -358,7 +358,6 @@ def tile_efficientattention_pa_kernel(tc, x, Wq, Wk, Wv, out_0, out_1, out_2):
                 banks[step] = transposes(step)
             for step in t_steps:
                 grouped[step] = copies(step, banks[step])
-            for step in t_steps:
                 for s_step, i0, i1 in SORT_PLAN.get(step, []):
                     reorder(s_step, i0, i1)
                 if step + RAW_BUFS < N_T:

import math
from contextlib import ExitStack

import concourse.mybir as mybir
from concourse.masks import make_identity

S, H, NH, NKV, HD = 512, 2048, 16, 4, 128
FLOPS = 2 * S * H * (NH + 2 * NKV) * HD

F32 = mybir.dt.float32
BF16 = mybir.dt.bfloat16
I32 = mybir.dt.int32
U32 = mybir.dt.uint32
U8 = mybir.dt.uint8
E5X4 = mybir.dt.float8_e5m2_x4
ALU = mybir.AluOpType
ACT = mybir.ActivationFunctionType

P = 128
PASSES = 4
GROUPS = 6
N_T = 2 + 2 * GROUPS
N_MM = 2 * GROUPS
LAG = 4
RAW_BUFS = 8
R0 = 5
R_TILES = 3
R_FULL = 8
SORT_PLAN = {
    4: [(5, 0, 2), (5, 2, 3)],
    5: [(6, 0, 2), (7, 0, 2)],
    6: [(8, 0, 3)],
    7: [(9, 0, 3)],
    8: [(10, 0, 3)],
    9: [(11, 0, 3)],
    10: [(12, 0, 3)],
    11: [(13, 0, 3)],
}
V_SORT = {6: [8], 8: [10], 10: [12]}
SORTED = {5: 3, 6: 2, 7: 2, 8: 4, 9: 3, 10: 4, 11: 3, 12: 4, 13: 3}
V_BANK_LAST = 3
PHASES = [([0], []), ([1], []), ([2], []), ([3], []), ([4], [0]), ([5], [1]), ([6, 7], [2, 3]), ([8, 9], [4, 5]), ([10, 11], [6, 7]), ([12, 13], [8, 9]), ([], [10]), ([], [11])]
SPLIT_LAST = 5
V_ADDS = [9]
G_HEADS = 3
N_WARM = 6
X_STEPS = [0, 1]
MM_EARLY = {4: 0, 5: 1}
HALF = 64
RATIO = 10000.0 ** (-1.0 / 64.0)
TWO_PI = 2.0 * math.pi
C1 = 6.28125
C2 = TWO_PI - C1


def tile_efficientattention_pa_kernel(tc, x, Wq, Wk, Wv, out_0, out_1, out_2):
    nc = tc.nc
    with ExitStack() as ctx:
        ctx.enter_context(tc.manual_schedule())
        const = ctx.enter_context(tc.tile_pool(name="const", bufs=1))
        raw = ctx.enter_context(tc.tile_pool(name="raw", bufs=RAW_BUFS))
        stage = ctx.enter_context(tc.tile_pool(name="stage", bufs=3))
        wq_pool = ctx.enter_context(tc.tile_pool(name="wq_pool", bufs=3))
        work = ctx.enter_context(tc.tile_pool(name="work", bufs=2))
        psum = ctx.enter_context(tc.psum_pool(name="psum", bufs=8))

        xv = x.flatten_outer_dims().rearrange("(r a) k -> r a k", a=4)
        raw_tiles = {}

        def w_of(step):
            w = step - 1 if step < X_STEPS[1] else step - 2
            return w // 2, w % 2

        def load(step):
            if step in X_STEPS:
                t = raw.tile([P, 2, 2048], BF16, name="raw_t", tag="raw_t")
                raw_tiles[step] = t
                a0 = 2 * X_STEPS.index(step)
                if step == 0:
                    nc.sync.dma_start(out=t[:, 0, 0:1024], in_=xv[:, a0, 0:1024])
                    nc.sync.dma_start(out=t[:, 0, 1024:2048], in_=xv[:, a0, 1024:2048])
                else:
                    nc.sync.dma_start(out=t[:, 0, :], in_=xv[:, a0, :])
                nc.sync.dma_start(out=t[:, 1, :], in_=xv[:, a0 + 1, :])
                return
            t = raw.tile([P, 4, 1024], BF16, name="raw_t", tag="raw_t")
            raw_tiles[step] = t
            n, gp = w_of(step)
            if n < 4:
                src = Wq[512 * n : 512 * (n + 1), :]
            elif n == 4:
                src = Wk
            else:
                src = Wv
            view = src.rearrange("(i d) k -> d i k", i=4)[:, :, 1024 * gp : 1024 * (gp + 1)]
            if step <= SPLIT_LAST:
                for ip in range(2):
                    nc.sync.dma_start(out=t[:, 2 * ip : 2 * ip + 2, :], in_=view[:, 2 * ip : 2 * ip + 2, :])
            else:
                nc.sync.dma_start(out=t[:], in_=view)

        for step in range(RAW_BUFS):
            load(step)

        wz = const.tile([P, 512], BF16, name="wz", tag="wz")
        nc.vector.memset(wz[:], 0.0)
        for w in range(N_WARM):
            wacc = psum.tile([P, 512], F32, name="bank", tag="bank")
            nc.tensor.matmul(out=wacc[:], lhsT=wz[:, 0:P], rhs=wz[:], start=True, stop=True)

        ident = const.tile([P, P], F32, name="ident", tag="ident")
        make_identity(nc, ident[:])
        zero1 = const.tile([P, 1], F32, name="zero1", tag="zero1")
        nc.vector.memset(zero1[:], 0.0)
        warm = const.tile([P, 1], F32, name="warm", tag="warm")
        nc.scalar.activation(out=warm[:], in_=zero1[:], func=ACT.Sin)

        pos_i = const.tile([P, 4], I32, name="pos_i", tag="pos_i")
        nc.gpsimd.iota(pos_i[:], pattern=[[1, 4]], base=0, channel_multiplier=4)
        pos = const.tile([P, 4], F32, name="pos", tag="pos")
        nc.vector.tensor_copy(out=pos[:], in_=pos_i[:])
        ones = const.tile([P, 8], F32, name="ones", tag="ones")
        nc.vector.memset(ones[:], 1.0)
        fa = const.tile([P, 8, 8], F32, name="fa", tag="fa")
        fb = const.tile([P, 8, 8], F32, name="fb", tag="fb")
        for j in range(8):
            nc.vector.tensor_scalar(out=fa[:, j, :], in0=ones[:], scalar1=RATIO ** (8 * j), scalar2=None, op0=ALU.mult)
            nc.vector.tensor_scalar(out=fb[:, :, j], in0=ones[:], scalar1=RATIO ** j, scalar2=None, op0=ALU.mult)
        freq = const.tile([P, HALF], F32, name="freq", tag="freq")
        nc.vector.tensor_tensor(
            out=freq[:], in0=fa[:].rearrange("p a b -> p (a b)"), in1=fb[:].rearrange("p a b -> p (a b)"), op=ALU.mult
        )
        ang = const.tile([P, 4, HALF], F32, name="ang", tag="ang")
        for a in range(4):
            nc.vector.tensor_scalar(out=ang[:, a, :], in0=freq[:], scalar1=pos[:, a : a + 1], scalar2=None, op0=ALU.mult)
        angf = ang[:].rearrange("p a j -> p (a j)")
        turns_i = const.tile([P, 4 * HALF], I32, name="turns_i", tag="turns_i")
        nc.vector.tensor_scalar(out=turns_i[:], in0=angf, scalar1=1.0 / TWO_PI, scalar2=None, op0=ALU.mult)
        turns = const.tile([P, 4 * HALF], F32, name="turns", tag="turns")
        nc.vector.tensor_copy(out=turns[:], in_=turns_i[:])
        r1 = const.tile([P, 4 * HALF], F32, name="r1", tag="r1")
        nc.vector.scalar_tensor_tensor(out=r1[:], in0=turns[:], scalar=-C1, in1=angf, op0=ALU.mult, op1=ALU.add)
        r2 = const.tile([P, 4 * HALF], F32, name="r2", tag="r2")
        nc.vector.scalar_tensor_tensor(out=r2[:], in0=turns[:], scalar=-C2, in1=r1[:], op0=ALU.mult, op1=ALU.add)
        m1 = const.tile([P, 4 * HALF], F32, name="m1", tag="m1")
        nc.vector.tensor_scalar(out=m1[:], in0=r2[:], scalar1=math.pi, scalar2=-TWO_PI, op0=ALU.is_gt, op1=ALU.mult)
        r3 = const.tile([P, 4 * HALF], F32, name="r3", tag="r3")
        nc.vector.tensor_tensor(out=r3[:], in0=r2[:], in1=m1[:], op=ALU.add)
        m2 = const.tile([P, 4 * HALF], F32, name="m2", tag="m2")
        nc.vector.tensor_scalar(out=m2[:], in0=r3[:], scalar1=-math.pi, scalar2=TWO_PI, op0=ALU.is_lt, op1=ALU.mult)
        r4 = const.tile([P, 4, HALF], F32, name="r4", tag="r4")
        r4f = r4[:].rearrange("p a j -> p (a j)")
        nc.vector.tensor_tensor(out=r4f, in0=r3[:], in1=m2[:], op=ALU.add)
        absr = const.tile([P, 4, HALF], F32, name="absr", tag="absr")
        nc.vector.scalar_tensor_tensor(
            out=absr[:].rearrange("p a j -> p (a j)"), in0=r4f, scalar=-1.0, in1=r4f, op0=ALU.mult, op1=ALU.max
        )
        cs_tab = const.tile([P, 4, 2, 2, HALF], F32, name="cs_tab", tag="cs_tab")

        def finish_tables():
            nc.scalar.activation(out=cs_tab[:, :, 1, 0, :], in_=r4[:], func=ACT.Sin)
            nc.scalar.activation(out=cs_tab[:, :, 1, 1, :], in_=r4[:], func=ACT.Sin, scale=-1.0)
            for t in range(2):
                nc.scalar.activation(out=cs_tab[:, :, 0, t, :], in_=absr[:], func=ACT.Sin, scale=-1.0, bias=math.pi / 2.0)

        xc_tile = const.tile([P, 32 + 2048], U32, name="x_codes", tag="x_codes", align_bytes=256)
        xs_tile = const.tile([P, 192 + 2048], U8, name="x_scales", tag="x_scales", align_bytes=256)
        x_codes = xc_tile[:, 32:].rearrange("p (a g c) -> p a g c", a=2, g=PASSES)
        x_scales = xs_tile[:, 192:].rearrange("p (a g c) -> p a g c", a=2, g=PASSES)
        w_codes = {}
        w_scales = {}
        o_tiles = {}
        prods = {}

        ro_tiles = {}

        def reorder(step, i0, i1, on_vector=False):
            if step not in ro_tiles:
                ro = stage.tile([P, 2, 8, P], F32, name="ro", tag="ro")
                ro_tiles[step] = ro
            copy = nc.vector.tensor_copy if on_vector else nc.scalar.copy
            copy(
                out=ro_tiles[step][:, :, 2 * i0 : 2 * i1, :].rearrange("p u b (c j) -> p (b c) u j", j=4),
                in_=raw_tiles[step][:].bitcast(F32)[:, i0:i1, :].rearrange("p i (c j u) -> p (i c) u j", j=4, u=2),
            )

        def words(step, gl, i, u):
            if i < SORTED.get(step, 0):
                return ro_tiles[step][:, u, 2 * i + gl, :]
            return raw_tiles[step][:].bitcast(F32)[:, i, 256 * gl + u : 256 * (gl + 1) : 2]

        def transposes(step):
            banks = {}
            order = [(gl, ip) for gl in range(2) for ip in range(2)]
            if step <= SPLIT_LAST:
                order = [(gl, ip) for ip in range(2) for gl in range(2)]
            for gl, ip in order:
                tp = psum.tile([P, 2, 2, P], F32, name="bank", tag="bank")
                for il in range(2):
                    for u in range(2):
                        if step in X_STEPS:
                            g = 2 * gl + il
                            src = raw_tiles[step][:].bitcast(F32)[:, ip, 256 * g + u : 256 * (g + 1) : 2]
                        else:
                            src = words(step, gl, 2 * ip + il, u)
                        nc.tensor.transpose(tp[:, il, u, :], src, ident[:])
                banks[(gl, ip)] = tp
            return order, banks

        def copies(step, banks):
            gt = stage.tile([P, 4096], BF16, name="grouped", tag="grouped", align_bytes=64)
            gw = gt[:].bitcast(F32).rearrange("p (g i r u) -> p g i r u", g=2, i=4, u=2)
            gx = gt[:].bitcast(F32).rearrange("p (g i r u) -> p g i r u", g=4, i=2, u=2)
            order, tiles = banks
            for gl, ip in order:
                src = tiles[(gl, ip)][:].rearrange("p i u r -> p i r u")
                dst = gx[:, 2 * gl : 2 * gl + 2, ip] if step in X_STEPS else gw[:, gl, 2 * ip : 2 * ip + 2]
                if step <= V_BANK_LAST and ip == 1 and gl == 1:
                    nc.vector.tensor_copy(out=dst, in_=src)
                else:
                    nc.scalar.copy(out=dst, in_=src)
            return gt

        def quantize(step, grouped):
            if step in X_STEPS:
                half = X_STEPS.index(step)
                nc.vector.quantize_mx(
                    out=x_codes[:, half, :, :].rearrange("p g c -> p (g c)").bitcast(E5X4),
                    scales=x_scales[:, half, :, :].rearrange("p g c -> p (g c)"),
                    in_=grouped[:],
                )
                return
            if True:
                n, gp = w_of(step)
                g0 = 2 * gp
                if g0 == 0:
                    wc = wq_pool.tile([P, PASSES, 512], U32, name="w_codes", tag="w_codes", align_bytes=256)
                    ws = wq_pool.tile([P, 64 + PASSES * 512], U8, name="w_scales", tag="w_scales", align_bytes=256)
                    w_codes[n] = wc
                    w_scales[n] = ws[:, 64:].rearrange("p (g c) -> p g c", g=PASSES)
                codes, scales = w_codes[n], w_scales[n]
            nc.vector.quantize_mx(
                out=codes[:, g0 : g0 + 2, :].rearrange("p g c -> p (g c)").bitcast(E5X4),
                scales=scales[:, g0 : g0 + 2, :].rearrange("p g c -> p (g c)"),
                in_=grouped[:],
            )

        def matmuls(mm):
            n, ap = mm // 2, mm % 2
            accs = []
            for al in range(2):
                a = 2 * ap + al
                acc = psum.tile([P, 512], F32, name="bank", tag="bank")
                for g in range(PASSES):
                    nc.tensor.matmul_mx(
                        out=acc[:],
                        lhsT=x_codes[:, ap, g, P * al : P * (al + 1)].bitcast(E5X4),
                        lhsT_scale=x_scales[:, ap, g, P * al : P * (al + 1)],
                        rhs=w_codes[n][:, g, :].bitcast(E5X4),
                        rhs_scale=w_scales[n][:, g, :],
                        start=(g == 0),
                        stop=(g == PASSES - 1),
                    )
                accs.append(acc)
            return accs

        def out_view(n):
            if n < 4:
                return out_0.rearrange("b h (r a) d -> r (b h) a d", a=4)[:, 4 * n : 4 * n + 4]
            if n == 4:
                return out_1.rearrange("b h (r a) d -> r (b h) a d", a=4)
            return out_2.rearrange("b h (r a) d -> r (b h) a d", a=4)

        def products(mm, accs):
            n, ap = mm // 2, mm % 2
            if ap == 0:
                ot = work.tile([P, 4, 4, HD], F32, name="o_tile", tag="o_tile", bufs=3)
                o_tiles[n] = ot
            if n == GROUPS - 1:
                nc.scalar.copy(out=o_tiles[n][:, :, 2 * ap, :], in_=accs[0][:].rearrange("p (h d) -> p h d", h=4))
                nc.scalar.dma_start(out=out_view(n)[:, :, 2 * ap, :], in_=o_tiles[n][:, :, 2 * ap, :])
                nc.scalar.copy(out=o_tiles[n][:, :, 2 * ap + 1, :], in_=accs[1][:].rearrange("p (h d) -> p h d", h=4))
                nc.scalar.dma_start(out=out_view(n)[:, :, 2 * ap + 1, :], in_=o_tiles[n][:, :, 2 * ap + 1, :])
                return
            pr = work.tile([P, 2, 2, 512], F32, name="prod", tag="prod", bufs=3)
            prods[mm] = pr
            last_rope = n == GROUPS - 2
            for al in range(2):
                a = 2 * ap + al
                nc.vector.tensor_tensor(
                    out=pr[:, al, :, :].rearrange("p c (h d) -> p c h d", d=HD),
                    in0=cs_tab[:, a, :, :, :].rearrange("p c t j -> p c (t j)").unsqueeze(2).to_broadcast([P, 2, 4, HD]),
                    in1=accs[al][:].rearrange("p (h d) -> p h d", d=HD).unsqueeze(1).to_broadcast([P, 2, 4, HD]),
                    op=ALU.mult,
                )
                if mm in V_ADDS:
                    if al == 1:
                        for t in range(2):
                            add(nc.vector, mm, 0, 2, t)
                else:
                    head_add(nc.gpsimd, mm, al, al + 1, 0, G_HEADS)
                if al == 0 and mm >= 1:
                    head_add(nc.vector, mm - 1, 0, 2, G_HEADS, 4)
                    sums(mm - 1)
            if mm in V_ADDS:
                sums(mm)

        def head_add(eng, mm, al0, al1, h0, h1):
            n, ap = mm // 2, mm % 2
            prv = prods[mm][:].rearrange("p a c (h t j) -> p a c h t j", h=4, t=2)
            ov = o_tiles[n][:].rearrange("p h a (t j) -> p a h t j", t=2)
            if al1 - al0 == 1:
                eng.tensor_tensor(
                    out=ov[:, 2 * ap + al0, h0:h1, :, :],
                    in0=prv[:, al0, 0, h0:h1, :, :],
                    in1=prv[:, al0, 1, h0:h1, ::-1, :],
                    op=ALU.add,
                )
            else:
                eng.tensor_tensor(
                    out=ov[:, 2 * ap + al0 : 2 * ap + al1, h0, :, :],
                    in0=prv[:, al0:al1, 0, h0, :, :],
                    in1=prv[:, al0:al1, 1, h0, ::-1, :],
                    op=ALU.add,
                )

        def add(eng, mm, al0, al1, t):
            n, ap = mm // 2, mm % 2
            prv = prods[mm][:].rearrange("p a c (h t j) -> p a c h t j", h=4, t=2)
            ov = o_tiles[n][:].rearrange("p h a (t j) -> p a h t j", t=2)
            eng.tensor_tensor(
                out=ov[:, 2 * ap + al0 : 2 * ap + al1, :, t, :],
                in0=prv[:, al0:al1, 0, :, t, :],
                in1=prv[:, al0:al1, 1, :, 1 - t, :],
                op=ALU.add,
            )

        def sums(mm):
            n, ap = mm // 2, mm % 2
            if mm < 0 or n == GROUPS - 1:
                return
            last_rope = n == GROUPS - 2
            if last_rope:
                nc.sync.dma_start(
                    out=out_view(n)[:, :, 2 * ap : 2 * ap + 2, :].rearrange("r h a d -> r h (a d)"),
                    in_=o_tiles[n][:, :, 2 * ap : 2 * ap + 2, :].rearrange("p h a d -> p h (a d)"),
                )
            elif ap == 1:
                nc.sync.dma_start(
                    out=out_view(n).rearrange("r h a d -> r h (a d)"),
                    in_=o_tiles[n][:].rearrange("p h a d -> p h (a d)"),
                )

        for t_steps, units in PHASES:
            banks = {}
            grouped = {}
            for step in t_steps:
                banks[step] = transposes(step)
            for step in t_steps:
                grouped[step] = copies(step, banks[step])
                for s_step, i0, i1 in SORT_PLAN.get(step, []):
                    reorder(s_step, i0, i1)
                if step + RAW_BUFS < N_T:
                    load(step + RAW_BUFS)
            for slot in range(max(len(t_steps), len(units))):
                if slot < len(t_steps):
                    if t_steps[slot] == 1:
                        finish_tables()
                    quantize(t_steps[slot], grouped[t_steps[slot]])
                    for s_step in V_SORT.get(t_steps[slot], []):
                        reorder(s_step, 3, 4, on_vector=True)
                if slot < len(units):
                    accs = matmuls(units[slot])
                    products(units[slot], accs)
